import numpy as np
import ml_dtypes


def mxq(x, axis, fmt="e4m3"):
    dtype, down = {"e4m3": (ml_dtypes.float8_e4m3fn, 7), "e5m2": (ml_dtypes.float8_e5m2, 14)}[fmt]
    v = np.moveaxis(np.asarray(x, np.float32).astype(ml_dtypes.bfloat16).astype(np.float64), axis, -1)
    blocks = v.reshape(v.shape[:-1] + (-1, 32))
    amax = np.abs(blocks).max(-1, keepdims=True)
    byte = np.maximum(np.where(amax > 0, np.frexp(amax)[1] - 1 + 127, 0) - down, 1)
    scale = np.exp2(byte - 127.0)
    codes = (blocks / scale).astype(np.float32).astype(dtype).astype(np.float64)
    return np.moveaxis((codes * scale).reshape(v.shape), -1, axis)


WIDE = False


def mx_kscale(k):
    if not WIDE:
        return np.ones(k)
    levels = np.array([10, -10, 5, -5, 0])
    a = np.random.permutation(np.resize(levels, k // 512 * 4)).reshape(k // 512, 4)
    idx = np.arange(k)
    return np.exp2(a[idx // 512, idx % 128 // 32])


BF16 = ml_dtypes.bfloat16


def bf(x):
    return np.asarray(x, np.float32).astype(BF16)


def f64(x):
    return np.asarray(x).astype(np.float64)


E2M1 = np.array([0.0, 0.5, 1.0, 1.5, 2.0, 3.0, 4.0, 6.0, -0.0, -0.5, -1.0, -1.5, -2.0, -3.0, -4.0, -6.0])


def pack_weight(w, fmt):
    k, n = w.shape
    w = f64(bf(w)).reshape(k // 32, 32, n)
    amax = np.abs(w).max(1)
    if fmt == "e4m3":
        byte = np.frexp(amax)[1] - 1 + 127 - 7
    else:
        mant, ex = np.frexp(amax / 6.0)
        byte = np.where(mant > 0.5, ex, ex - 1) + 127
    byte = np.clip(np.where(amax > 0, byte, 1), 1, 254)
    scaled = (w * np.exp2(127.0 - byte)[:, None, :]).reshape(k, n).astype(np.float32)
    by_word = np.ascontiguousarray(scaled.reshape(k // 512, 128, 4, n).transpose(0, 1, 3, 2))
    if fmt == "e4m3":
        words = by_word.astype(ml_dtypes.float8_e4m3fn).view(np.uint8)
    else:
        c = by_word.astype(ml_dtypes.float4_e2m1fn).view(np.uint8) & 0xF
        words = c[..., 0::2] | (c[..., 1::2] << 4)
    return np.ascontiguousarray(words), np.ascontiguousarray(byte.astype(np.uint8).reshape(k // 512, 16, n))


def unpack_weight(words, scales, fmt):
    g, p, n, _ = words.shape
    if fmt == "e4m3":
        vals = np.ascontiguousarray(words).view(ml_dtypes.float8_e4m3fn).astype(np.float64)
    else:
        nib = np.empty((g, p, n, 4), np.uint8)
        nib[..., 0::2] = words & 0xF
        nib[..., 1::2] = words >> 4
        vals = E2M1[nib]
    vals = vals * np.repeat(np.exp2(scales.astype(np.float64) - 127.0), 8, axis=1)[..., None]
    return vals.transpose(0, 1, 3, 2).reshape(g * 512, n)


B, L, C, KS, NL, BH, R = 1, 128, 2048, 4, 16, 64, 2
OUT = 2 * BH * NL
FMT = "e4m3"


def setup_inputs():
    s, t = mx_kscale(C), mx_kscale(C)
    local_features = bf(np.random.standard_normal((B, L, C)) * s)
    wt = bf(np.random.standard_normal((C, C, KS)) / np.sqrt(C) / s[:, None, None] * t[None, :, None])
    bt = bf(np.random.standard_normal(C) * 0.5 * t)
    w1 = np.random.standard_normal((OUT, C)) / np.sqrt(C) / t[None, :]
    w1_words, w1_scales = pack_weight(np.ascontiguousarray(w1.T), FMT)
    b1 = bf(np.random.standard_normal(OUT) * 0.5)
    return {"local_features": local_features,
            "wt": wt,
            "bt": bt,
            "w1_words": w1_words,
            "w1_scales": w1_scales,
            "b1": b1}


def reference(local_features, wt, bt, w1_words, w1_scales, b1):
    xq = mxq(f64(local_features), 2, "e4m3")
    wq = mxq(f64(wt), 0, "e4m3")
    up = xq @ wq.reshape(C, C * KS)
    up = up.reshape(B, L, C, KS).transpose(0, 2, 1, 3).reshape(B, C, L * KS) + f64(bt)[None, :, None]
    y = (unpack_weight(w1_words, w1_scales, FMT).T @ mxq(up, 1, "e4m3")) + f64(b1)[None, :, None]
    y = np.tile(y, (1, 1, R))
    y = y.reshape(B, NL, 2 * BH, L * KS * R)
    return np.ascontiguousarray(y.transpose(2, 0, 1, 3))

@@ -1,0 +1,179 @@
+from contextlib import ExitStack
+
+import concourse.bass as bass
+import concourse.mybir as mybir
+import concourse.tile as tile
+from concourse.masks import make_identity
+
+BF16 = mybir.dt.bfloat16
+F32 = mybir.dt.float32
+I32 = mybir.dt.int32
+U32 = mybir.dt.uint32
+U8 = mybir.dt.uint8
+FP8X4 = mybir.dt.float8_e4m3fn_x4
+ADD = mybir.AluOpType.add
+IDENT = mybir.ActivationFunctionType.Identity
+
+P = 128
+L = 128
+C = 2048
+KS = 4
+G = 4
+T = L * KS
+NT = 16
+
+FLOPS = 2 * L * C * C * KS + 2 * C * C * T
+
+V_UNITS = ((1, 3), (1, 3), (1, 3), (3,))
+
+
+def tile_conditionalfeaturesupsample_w_kernel(tc, local_features, wt, bt, w1_words, w1_scales, b1, out):
+    nc = tc.nc
+    with ExitStack() as ctx:
+        keep = ctx.enter_context(tc.tile_pool(name="keep", bufs=1))
+        rawp = ctx.enter_context(tc.tile_pool(name="rawp", bufs=3))
+        grpp = ctx.enter_context(tc.tile_pool(name="grpp", bufs=4))
+        codp = ctx.enter_context(tc.tile_pool(name="codp", bufs=6))
+        upp = ctx.enter_context(tc.tile_pool(name="upp", bufs=2))
+        outp = ctx.enter_context(tc.tile_pool(name="outp", bufs=3))
+        psum = ctx.enter_context(tc.psum_pool(name="psum", bufs=8))
+
+        planes = keep.tile([P, C], U8, align_bytes=64)
+        nc.vector.memset(planes[:].bitcast(I32), 0)
+        b1_rows = keep.tile([P, P], BF16)
+        nc.vector.memset(b1_rows[:], 0.0)
+        ident = keep.tile([P, P], F32)
+        make_identity(nc, ident[:])
+
+        x_sb = keep.tile([P, C], BF16)
+        nc.sync.dma_start(out=x_sb[:], in_=local_features[0])
+        for q in range(4):
+            nc.sync.dma_start(
+                out=planes[32 * q : 32 * q + 16, :].bitcast(I32),
+                in_=w1_scales[:, 4 * q : 4 * q + 4, :].bitcast(I32),
+            )
+        bt_bf = keep.tile([P, G, 4], BF16)
+        nc.scalar.dma_start(out=bt_bf[:], in_=bt.rearrange("(g p j) -> p g j", g=G, p=P, j=4))
+        nc.scalar.dma_start(out=b1_rows[0:NT, :], in_=b1.rearrange("(n j) -> n j", j=P))
+
+        bt_f = keep.tile([P, G, 4], F32)
+        nc.vector.tensor_copy(out=bt_f[:], in_=bt_bf[:])
+        b1_rows_f = keep.tile([P, P], F32)
+        nc.vector.tensor_copy(out=b1_rows_f[:], in_=b1_rows[:])
+
+        x_words = x_sb[:].bitcast(F32)
+        gx = keep.tile([P, G, L, 4], BF16, align_bytes=64)
+        gx_words = gx[:].bitcast(F32)
+        for h in range(2):
+            xt = psum.tile([P, 2, 2, L], F32, tag="bank")
+            for g2 in range(2):
+                gc = 2 * h + g2
+                for u in range(2):
+                    nc.tensor.transpose(xt[:, g2, u, :], x_words[:, 256 * gc + u : 256 * (gc + 1) : 2], ident[:])
+            nc.vector.tensor_copy(
+                out=gx_words[:, 2 * h : 2 * h + 2, :, :], in_=xt[:].rearrange("p g u l -> p g l u")
+            )
+        b1_ps = psum.tile([P, P], F32, tag="bank")
+        nc.tensor.transpose(b1_ps[:], b1_rows_f[:], ident[:])
+        b1_f = keep.tile([P, NT], F32)
+        nc.vector.tensor_copy(out=b1_f[:], in_=b1_ps[:, 0:NT])
+
+        x_codes = keep.tile([P, G, L], U32, align_bytes=64)
+        x_scales = keep.tile([P, G, L], U8, align_bytes=64)
+        nc.vector.quantize_mx(
+            out=x_codes[:].rearrange("p g l -> p (g l)").bitcast(FP8X4),
+            scales=x_scales[:].rearrange("p g l -> p (g l)"),
+            in_=gx[:].rearrange("p g l t -> p (g l t)"),
+        )
+
+        up_codes = keep.tile([P, G, T], U32, align_bytes=64)
+        up_scales = keep.tile([P, G, T], U8, align_bytes=64)
+        w1w = keep.tile([P, G, C], U32, align_bytes=64)
+
+        for go in range(G):
+            codes = []
+            scales = []
+            for gc in range(G):
+                raw = rawp.tile([P, 4, 4 * 512], BF16, tag="raw")
+                nc.sync.dma_start(
+                    out=raw[:],
+                    in_=wt[512 * gc : 512 * (gc + 1), 512 * go : 512 * (go + 1), :].rearrange(
+                        "(p j) o k -> p j (o k)", j=4
+                    ),
+                )
+                raw_v = raw[:].rearrange("p j (q a k) -> p a q j k", a=4, k=KS)
+                cod = codp.tile([P, 16, P], U32, tag="cod", align_bytes=64)
+                scl = codp.tile([P, 16, P], U8, tag="scl", align_bytes=64)
+                for h in range(2):
+                    gh = grpp.tile([P, 8, P, 4], BF16, tag="gh", align_bytes=64)
+                    for a in range(2):
+                        j2 = 2 * h + a
+                        dst = gh[:, 4 * a : 4 * a + 4, :, :].rearrange("p k q j -> p q j k")
+                        if j2 in V_UNITS[gc]:
+                            nc.vector.tensor_copy(out=dst, in_=raw_v[:, j2])
+                        else:
+                            nc.scalar.copy(out=dst, in_=raw_v[:, j2])
+                    nc.vector.quantize_mx(
+                        out=cod[:, 8 * h : 8 * h + 8, :].rearrange("p s q -> p (s q)").bitcast(FP8X4),
+                        scales=scl[:, 8 * h : 8 * h + 8, :].rearrange("p s q -> p (s q)"),
+                        in_=gh[:].rearrange("p s q j -> p (s q j)"),
+                    )
+                codes.append(cod)
+                scales.append(scl)
+
+            g2t = upp.tile([P, KS, L, 4], BF16, tag="g2t", align_bytes=64)
+            for k in range(KS):
+                ps1 = psum.tile([P, 4, L], F32, tag="bank")
+                for j2 in range(4):
+                    s = 4 * j2 + k
+                    for gc in range(G):
+                        nc.tensor.matmul_mx(
+                            out=ps1[:, j2, :],
+                            lhsT=codes[gc][:, s, :].bitcast(FP8X4),
+                            lhsT_scale=scales[gc][:, s, :],
+                            rhs=x_codes[:, gc, :].bitcast(FP8X4),
+                            rhs_scale=x_scales[:, gc, :],
+                            start=(gc == 0),
+                            stop=(gc == G - 1),
+                        )
+                nc.vector.tensor_tensor(
+                    out=g2t[:, k, :, :],
+                    in0=ps1[:].rearrange("p j l -> p l j"),
+                    in1=bt_f[:, go, :].unsqueeze(1).to_broadcast([P, L, 4]),
+                    op=ADD,
+                )
+            nc.vector.quantize_mx(
+                out=up_codes[:, go, :].bitcast(FP8X4),
+                scales=up_scales[:, go, :],
+                in_=g2t[:].rearrange("p k l j -> p (k l j)"),
+            )
+
+        w1_src = w1_words.rearrange("g p n t -> p g (n t)").bitcast(I32)
+        for h in range(2):
+            nc.sync.dma_start(
+                out=w1w[:, :, 1024 * h : 1024 * (h + 1)].bitcast(I32), in_=w1_src[:, :, 1024 * h : 1024 * (h + 1)]
+            )
+
+        out_v = out.rearrange("j b n t -> j (b n) t")
+        for pair in range(NT // 2):
+            y = outp.tile([P, 2, 2 * T], F32, tag="y")
+            for i in range(2):
+                n = 2 * pair + i
+                ps2 = psum.tile([P, T], F32, tag="bank")
+                for g in range(G):
+                    nc.tensor.matmul_mx(
+                        out=ps2[:],
+                        lhsT=w1w[:, g, P * n : P * (n + 1)].bitcast(FP8X4),
+                        lhsT_scale=planes[4 * g : P, P * n : P * (n + 1)],
+                        rhs=up_codes[:, g, :].bitcast(FP8X4),
+                        rhs_scale=up_scales[:, g, :],
+                        start=(g == 0),
+                        stop=(g == G - 1),
+                    )
+                src = ps2[:].rearrange("p (k l) -> p l k", k=KS).unsqueeze(1).to_broadcast([P, 2, L, KS])
+                dst = y[:, i, :].rearrange("p (r l k) -> p r l k", r=2, k=KS)
+                if i == 0:
+                    nc.scalar.activation(out=dst, in_=src, func=IDENT, bias=b1_f[:, n : n + 1])
+                else:
+                    nc.vector.tensor_scalar(out=dst, in0=src, scalar1=b1_f[:, n : n + 1], scalar2=None, op0=ADD)
+            nc.sync.dma_start(out=out_v[:, 2 * pair : 2 * pair + 2, :], in_=y[:])

@@ -1,8 +1,6 @@
 from contextlib import ExitStack
 
-import concourse.bass as bass
 import concourse.mybir as mybir
-import concourse.tile as tile
 from concourse.masks import make_identity
 
 BF16 = mybir.dt.bfloat16
@@ -21,21 +19,24 @@ KS = 4
 G = 4
 T = L * KS
 NT = 16
+W = 2048
+NB = 512
+CHUNKS = G * G
+V_COLS = 960
 
 FLOPS = 2 * L * C * C * KS + 2 * C * C * T
-
-V_UNITS = ((1, 3), (1, 3), (1, 3), (3,))
 
 
 def tile_conditionalfeaturesupsample_w_kernel(tc, local_features, wt, bt, w1_words, w1_scales, b1, out):
     nc = tc.nc
     with ExitStack() as ctx:
+        ctx.enter_context(tc.manual_schedule())
         keep = ctx.enter_context(tc.tile_pool(name="keep", bufs=1))
-        rawp = ctx.enter_context(tc.tile_pool(name="rawp", bufs=3))
+        rawp = ctx.enter_context(tc.tile_pool(name="rawp", bufs=4))
         grpp = ctx.enter_context(tc.tile_pool(name="grpp", bufs=4))
-        codp = ctx.enter_context(tc.tile_pool(name="codp", bufs=6))
+        codp = ctx.enter_context(tc.tile_pool(name="codp", bufs=4))
         upp = ctx.enter_context(tc.tile_pool(name="upp", bufs=2))
-        outp = ctx.enter_context(tc.tile_pool(name="outp", bufs=3))
+        outp = ctx.enter_context(tc.tile_pool(name="outp", bufs=5))
         psum = ctx.enter_context(tc.psum_pool(name="psum", bufs=8))
 
         planes = keep.tile([P, C], U8, align_bytes=64)
@@ -46,99 +47,97 @@ def tile_conditionalfeaturesupsample_w_kernel(tc, local_features, wt, bt, w1_wor
         make_identity(nc, ident[:])
 
         x_sb = keep.tile([P, C], BF16)
-        nc.sync.dma_start(out=x_sb[:], in_=local_features[0])
-        for q in range(4):
-            nc.sync.dma_start(
-                out=planes[32 * q : 32 * q + 16, :].bitcast(I32),
-                in_=w1_scales[:, 4 * q : 4 * q + 4, :].bitcast(I32),
-            )
         bt_bf = keep.tile([P, G, 4], BF16)
-        nc.scalar.dma_start(out=bt_bf[:], in_=bt.rearrange("(g p j) -> p g j", g=G, p=P, j=4))
-        nc.scalar.dma_start(out=b1_rows[0:NT, :], in_=b1.rearrange("(n j) -> n j", j=P))
-
         bt_f = keep.tile([P, G, 4], F32)
-        nc.vector.tensor_copy(out=bt_f[:], in_=bt_bf[:])
         b1_rows_f = keep.tile([P, P], F32)
-        nc.vector.tensor_copy(out=b1_rows_f[:], in_=b1_rows[:])
-
-        x_words = x_sb[:].bitcast(F32)
-        gx = keep.tile([P, G, L, 4], BF16, align_bytes=64)
-        gx_words = gx[:].bitcast(F32)
-        for h in range(2):
-            xt = psum.tile([P, 2, 2, L], F32, tag="bank")
-            for g2 in range(2):
-                gc = 2 * h + g2
-                for u in range(2):
-                    nc.tensor.transpose(xt[:, g2, u, :], x_words[:, 256 * gc + u : 256 * (gc + 1) : 2], ident[:])
-            nc.vector.tensor_copy(
-                out=gx_words[:, 2 * h : 2 * h + 2, :, :], in_=xt[:].rearrange("p g u l -> p g l u")
-            )
-        b1_ps = psum.tile([P, P], F32, tag="bank")
-        nc.tensor.transpose(b1_ps[:], b1_rows_f[:], ident[:])
         b1_f = keep.tile([P, NT], F32)
-        nc.vector.tensor_copy(out=b1_f[:], in_=b1_ps[:, 0:NT])
-
+        gx = keep.tile([P, G, L, 4], BF16, align_bytes=64)
         x_codes = keep.tile([P, G, L], U32, align_bytes=64)
         x_scales = keep.tile([P, G, L], U8, align_bytes=64)
-        nc.vector.quantize_mx(
-            out=x_codes[:].rearrange("p g l -> p (g l)").bitcast(FP8X4),
-            scales=x_scales[:].rearrange("p g l -> p (g l)"),
-            in_=gx[:].rearrange("p g l t -> p (g l t)"),
-        )
-
         up_codes = keep.tile([P, G, T], U32, align_bytes=64)
         up_scales = keep.tile([P, G, T], U8, align_bytes=64)
         w1w = keep.tile([P, G, C], U32, align_bytes=64)
+        w1_src = w1_words.rearrange("g p n t -> p g (n t)").bitcast(I32)
 
-        for go in range(G):
-            codes = []
-            scales = []
-            for gc in range(G):
-                raw = rawp.tile([P, 4, 4 * 512], BF16, tag="raw")
-                nc.sync.dma_start(
-                    out=raw[:],
-                    in_=wt[512 * gc : 512 * (gc + 1), 512 * go : 512 * (go + 1), :].rearrange(
-                        "(p j) o k -> p j (o k)", j=4
-                    ),
+        def load_chunk(c):
+            go, gc = divmod(c, G)
+            raw = rawp.tile([P, 4, W], BF16, tag="raw", name="raw")
+            src = wt[512 * gc : 512 * (gc + 1), 512 * go : 512 * (go + 1), :].rearrange("(p j) o k -> p j (o k)", j=4)
+            if c < 2:
+                for b in (0, 2, 1, 3):
+                    nc.sync.dma_start(out=raw[:, :, NB * b : NB * (b + 1)], in_=src[:, :, NB * b : NB * (b + 1)])
+            else:
+                nc.sync.dma_start(out=raw[:], in_=src)
+            return raw
+
+        def regroup(copy, raw, gh, lo, hi):
+            base = lo - lo % (2 * NB)
+            copy(
+                out=gh[:, lo - base : hi - base, :].rearrange("p (c i) t -> p c t i", i=4),
+                in_=raw[:, :, lo:hi].rearrange("p t (c i) -> p c t i", i=4),
+            )
+
+        def quantise(gh):
+            cod = codp.tile([P, 2 * NB], U32, tag="cod", name="cod", align_bytes=64)
+            scl = codp.tile([P, 2 * NB], U8, tag="scl", name="scl", align_bytes=64)
+            nc.vector.quantize_mx(out=cod[:].bitcast(FP8X4), scales=scl[:], in_=gh[:].rearrange("p w t -> p (w t)"))
+            return cod, scl
+
+        def passes(c, h, acc, cod, scl):
+            gc = c % G
+            for i in range(2):
+                if gc == 0:
+                    acc[2 * h + i] = psum.tile([P, NB], F32, tag="bank", name="acc")
+                nc.tensor.matmul_mx(
+                    out=acc[2 * h + i][:],
+                    lhsT=x_codes[:, gc, :].bitcast(FP8X4),
+                    lhsT_scale=x_scales[:, gc, :],
+                    rhs=cod[:, NB * i : NB * (i + 1)].bitcast(FP8X4),
+                    rhs_scale=scl[:, NB * i : NB * (i + 1)],
+                    start=(gc == 0),
+                    stop=(gc == G - 1),
                 )
-                raw_v = raw[:].rearrange("p j (q a k) -> p a q j k", a=4, k=KS)
-                cod = codp.tile([P, 16, P], U32, tag="cod", align_bytes=64)
-                scl = codp.tile([P, 16, P], U8, tag="scl", align_bytes=64)
-                for h in range(2):
-                    gh = grpp.tile([P, 8, P, 4], BF16, tag="gh", align_bytes=64)
-                    for a in range(2):
-                        j2 = 2 * h + a
-                        dst = gh[:, 4 * a : 4 * a + 4, :, :].rearrange("p k q j -> p q j k")
-                        if j2 in V_UNITS[gc]:
-                            nc.vector.tensor_copy(out=dst, in_=raw_v[:, j2])
-                        else:
-                            nc.scalar.copy(out=dst, in_=raw_v[:, j2])
-                    nc.vector.quantize_mx(
-                        out=cod[:, 8 * h : 8 * h + 8, :].rearrange("p s q -> p (s q)").bitcast(FP8X4),
-                        scales=scl[:, 8 * h : 8 * h + 8, :].rearrange("p s q -> p (s q)"),
-                        in_=gh[:].rearrange("p s q j -> p (s q j)"),
-                    )
-                codes.append(cod)
-                scales.append(scl)
 
-            g2t = upp.tile([P, KS, L, 4], BF16, tag="g2t", align_bytes=64)
+        def prepare_x():
+            x_words = x_sb[:].bitcast(F32)
+            gx_words = gx[:].bitcast(F32)
+            for h in range(2):
+                xt = psum.tile([P, 2, 2, L], F32, tag="bank", name="xt")
+                for g2 in range(2):
+                    gc = 2 * h + g2
+                    for u in range(2):
+                        nc.tensor.transpose(xt[:, g2, u, :], x_words[:, 256 * gc + u : 256 * (gc + 1) : 2], ident[:])
+                nc.vector.tensor_copy(out=gx_words[:, 2 * h : 2 * h + 2, :, :], in_=xt[:].rearrange("p g u l -> p g l u"))
+            nc.vector.tensor_copy(out=b1_rows_f[:], in_=b1_rows[:])
+            b1_ps = psum.tile([P, P], F32, tag="bank", name="b1_ps")
+            nc.tensor.transpose(b1_ps[:], b1_rows_f[:], ident[:])
+            nc.vector.quantize_mx(
+                out=x_codes[:].rearrange("p g l -> p (g l)").bitcast(FP8X4),
+                scales=x_scales[:].rearrange("p g l -> p (g l)"),
+                in_=gx[:].rearrange("p g l t -> p (g l t)"),
+            )
+            nc.vector.tensor_copy(out=b1_f[:], in_=b1_ps[:, 0:NT])
+            nc.vector.tensor_copy(out=bt_f[:], in_=bt_bf[:])
+
+        def turn(acc, last):
+            up_l = upp.tile([P, 16, P], F32, tag="up_l", name="up_l")
+            for b in range(4):
+                copy = nc.vector.tensor_copy if last and b == 3 else nc.scalar.copy
+                copy(out=up_l[:, :, 32 * b : 32 * (b + 1)], in_=acc[b][:].rearrange("p (q s) -> p s q", s=16))
+            banks = []
             for k in range(KS):
-                ps1 = psum.tile([P, 4, L], F32, tag="bank")
+                tb = psum.tile([P, 4, L], F32, tag="bank", name="tb")
                 for j2 in range(4):
-                    s = 4 * j2 + k
-                    for gc in range(G):
-                        nc.tensor.matmul_mx(
-                            out=ps1[:, j2, :],
-                            lhsT=codes[gc][:, s, :].bitcast(FP8X4),
-                            lhsT_scale=scales[gc][:, s, :],
-                            rhs=x_codes[:, gc, :].bitcast(FP8X4),
-                            rhs_scale=x_scales[:, gc, :],
-                            start=(gc == 0),
-                            stop=(gc == G - 1),
-                        )
+                    nc.tensor.transpose(tb[:, j2, :], up_l[:, 4 * j2 + k, :], ident[:])
+                banks.append(tb)
+            return banks
+
+        def finish_up(go, banks):
+            g2t = upp.tile([P, KS, L, 4], BF16, tag="g2t", name="g2t", align_bytes=64)
+            for k in range(KS):
                 nc.vector.tensor_tensor(
                     out=g2t[:, k, :, :],
-                    in0=ps1[:].rearrange("p j l -> p l j"),
+                    in0=banks[k][:].rearrange("p j l -> p l j"),
                     in1=bt_f[:, go, :].unsqueeze(1).to_broadcast([P, L, 4]),
                     op=ADD,
                 )
@@ -148,32 +147,74 @@ def tile_conditionalfeaturesupsample_w_kernel(tc, local_features, wt, bt, w1_wor
                 in_=g2t[:].rearrange("p k l j -> p (k l j)"),
             )
 
-        w1_src = w1_words.rearrange("g p n t -> p g (n t)").bitcast(I32)
-        for h in range(2):
-            nc.sync.dma_start(
-                out=w1w[:, :, 1024 * h : 1024 * (h + 1)].bitcast(I32), in_=w1_src[:, :, 1024 * h : 1024 * (h + 1)]
-            )
+        acc = [None, None, None, None]
+        old_acc = acc
+        banks = None
+        gh_s = None
+        waiting = []
+        for c in range(CHUNKS + 1):
+            if c < CHUNKS:
+                raw = load_chunk(c)
+                if c == 0:
+                    nc.sync.dma_start(out=x_sb[:], in_=local_features[0])
+                    nc.sync.dma_start(out=b1_rows[0:NT, :], in_=b1.rearrange("(n j) -> n j", j=P))
+                    nc.sync.dma_start(out=bt_bf[:], in_=bt.rearrange("(g p j) -> p g j", g=G, p=P, j=4))
+                if c == CHUNKS - 1:
+                    for q in range(4):
+                        nc.sync.dma_start(
+                            out=planes[32 * q : 32 * q + 16, :].bitcast(I32),
+                            in_=w1_scales[:, 4 * q : 4 * q + 4, :].bitcast(I32),
+                        )
+                    for g in range(G):
+                        nc.sync.dma_start(out=w1w[:, g, :].bitcast(I32), in_=w1_src[:, g, :])
+                gh_v = grpp.tile([P, 2 * NB, 4], BF16, tag="gh", name="gh_v", align_bytes=64)
+                if c < 2:
+                    regroup(nc.vector.tensor_copy, raw, gh_v, 0, NB)
+                    regroup(nc.vector.tensor_copy, raw, gh_v, NB, V_COLS)
+                else:
+                    regroup(nc.vector.tensor_copy, raw, gh_v, 0, V_COLS)
+            if c > 0:
+                waiting.append((c - 1, 1, quantise(gh_s)))
+            if c < CHUNKS:
+                gh_s = grpp.tile([P, 2 * NB, 4], BF16, tag="gh", name="gh_s", align_bytes=64)
+                regroup(nc.scalar.copy, raw, gh_s, 2 * NB, 3 * NB)
+                regroup(nc.scalar.copy, raw, gh_v, V_COLS, 2 * NB)
+                regroup(nc.scalar.copy, raw, gh_s, 3 * NB, 4 * NB)
+            if c == 1:
+                prepare_x()
+            if c > 1 and c % G == 1:
+                finish_up(c // G - 1, banks)
+            if c < CHUNKS:
+                waiting.append((c, 0, quantise(gh_v)))
+            if c > 0:
+                for cw, h, (cod, scl) in waiting:
+                    if cw % G == 0 and h == 0:
+                        old_acc = acc
+                        acc = [None, None, None, None]
+                    passes(cw, h, acc, cod, scl)
+                waiting = []
+            if c > 0 and c % G == 0:
+                banks = turn(old_acc if c < CHUNKS else acc, c == CHUNKS)
+        finish_up(G - 1, banks)
 
         out_v = out.rearrange("j b n t -> j (b n) t")
-        for pair in range(NT // 2):
-            y = outp.tile([P, 2, 2 * T], F32, tag="y")
-            for i in range(2):
-                n = 2 * pair + i
-                ps2 = psum.tile([P, T], F32, tag="bank")
-                for g in range(G):
-                    nc.tensor.matmul_mx(
-                        out=ps2[:],
-                        lhsT=w1w[:, g, P * n : P * (n + 1)].bitcast(FP8X4),
-                        lhsT_scale=planes[4 * g : P, P * n : P * (n + 1)],
-                        rhs=up_codes[:, g, :].bitcast(FP8X4),
-                        rhs_scale=up_scales[:, g, :],
-                        start=(g == 0),
-                        stop=(g == G - 1),
-                    )
-                src = ps2[:].rearrange("p (k l) -> p l k", k=KS).unsqueeze(1).to_broadcast([P, 2, L, KS])
-                dst = y[:, i, :].rearrange("p (r l k) -> p r l k", r=2, k=KS)
-                if i == 0:
-                    nc.scalar.activation(out=dst, in_=src, func=IDENT, bias=b1_f[:, n : n + 1])
-                else:
-                    nc.vector.tensor_scalar(out=dst, in0=src, scalar1=b1_f[:, n : n + 1], scalar2=None, op0=ADD)
-            nc.sync.dma_start(out=out_v[:, 2 * pair : 2 * pair + 2, :], in_=y[:])
+        for n in range(NT):
+            ps2 = psum.tile([P, T], F32, tag="bank", name="ps2")
+            for g in range(G):
+                nc.tensor.matmul_mx(
+                    out=ps2[:],
+                    lhsT=w1w[:, g, P * n : P * (n + 1)].bitcast(FP8X4),
+                    lhsT_scale=planes[4 * g : P, P * n : P * (n + 1)],
+                    rhs=up_codes[:, g, :].bitcast(FP8X4),
+                    rhs_scale=up_scales[:, g, :],
+                    start=(g == 0),
+                    stop=(g == G - 1),
+                )
+            y = outp.tile([P, 2 * T], F32, tag="y", name="y")
+            src = ps2[:].rearrange("p (k l) -> p l k", k=KS).unsqueeze(1).to_broadcast([P, 2, L, KS])
+            dst = y[:].rearrange("p (r l k) -> p r l k", r=2, k=KS)
+            if n % 2 == 0:
+                nc.scalar.activation(out=dst, in_=src, func=IDENT, bias=b1_f[:, n : n + 1])
+            else:
+                nc.vector.tensor_scalar(out=dst, in0=src, scalar1=b1_f[:, n : n + 1], scalar2=None, op0=ADD)
+            nc.sync.dma_start(out=out_v[:, n, :], in_=y[:])

@@ -22,7 +22,7 @@ NT = 16
 W = 2048
 NB = 512
 CHUNKS = G * G
-V_COLS = 960
+V_COLS = 1120
 
 FLOPS = 2 * L * C * C * KS + 2 * C * C * T
 
@@ -48,7 +48,10 @@ def tile_conditionalfeaturesupsample_w_kernel(tc, local_features, wt, bt, w1_wor
 
         x_sb = keep.tile([P, C], BF16)
         bt_bf = keep.tile([P, G, 4], BF16)
-        bt_f = keep.tile([P, G, 4], F32)
+        bt_pad = keep.tile([P, P], F32)
+        nc.vector.memset(bt_pad[:], 0.0)
+        bt_rows = keep.tile([P, P], BF16)
+        pick = keep.tile([P, 16, L], BF16)
         b1_rows_f = keep.tile([P, P], F32)
         b1_f = keep.tile([P, NT], F32)
         gx = keep.tile([P, G, L, 4], BF16, align_bytes=64)
@@ -59,13 +62,25 @@ def tile_conditionalfeaturesupsample_w_kernel(tc, local_features, wt, bt, w1_wor
         w1w = keep.tile([P, G, C], U32, align_bytes=64)
         w1_src = w1_words.rearrange("g p n t -> p g (n t)").bitcast(I32)
 
+        nc.scalar.dma_start(out=bt_bf[:], in_=bt.rearrange("(g p j) -> p g j", g=G, p=P, j=4))
+        nc.scalar.dma_start(out=b1_rows[0:NT, :], in_=b1.rearrange("(n j) -> n j", j=P))
+        nc.vector.tensor_copy(out=pick[:], in_=ident[:, 0:16].unsqueeze(2).to_broadcast([P, 16, L]))
+        nc.vector.tensor_copy(out=bt_pad[:, 0:16], in_=bt_bf[:].rearrange("p g j -> p (g j)"))
+        nc.vector.tensor_copy(out=b1_rows_f[:], in_=b1_rows[:])
+        bt_ps = psum.tile([P, P], F32, tag="bank", name="bt_ps")
+        nc.tensor.transpose(bt_ps[:], bt_pad[:], ident[:])
+        b1_ps = psum.tile([P, P], F32, tag="bank", name="b1_ps")
+        nc.tensor.transpose(b1_ps[:], b1_rows_f[:], ident[:])
+        nc.vector.tensor_copy(out=bt_rows[:], in_=bt_ps[:])
+        nc.vector.tensor_copy(out=b1_f[:], in_=b1_ps[:, 0:NT])
+
         def load_chunk(c):
             go, gc = divmod(c, G)
             raw = rawp.tile([P, 4, W], BF16, tag="raw", name="raw")
             src = wt[512 * gc : 512 * (gc + 1), 512 * go : 512 * (go + 1), :].rearrange("(p j) o k -> p j (o k)", j=4)
             if c < 2:
-                for b in (0, 2, 1, 3):
-                    nc.sync.dma_start(out=raw[:, :, NB * b : NB * (b + 1)], in_=src[:, :, NB * b : NB * (b + 1)])
+                for h in range(2):
+                    nc.sync.dma_start(out=raw[:, :, 2 * NB * h : 2 * NB * (h + 1)], in_=src[:, :, 2 * NB * h : 2 * NB * (h + 1)])
             else:
                 nc.sync.dma_start(out=raw[:], in_=src)
             return raw
@@ -77,10 +92,16 @@ def tile_conditionalfeaturesupsample_w_kernel(tc, local_features, wt, bt, w1_wor
                 in_=raw[:, :, lo:hi].rearrange("p t (c i) -> p c t i", i=4),
             )
 
-        def quantise(gh):
+        def quantise(gh, calls):
             cod = codp.tile([P, 2 * NB], U32, tag="cod", name="cod", align_bytes=64)
             scl = codp.tile([P, 2 * NB], U8, tag="scl", name="scl", align_bytes=64)
-            nc.vector.quantize_mx(out=cod[:].bitcast(FP8X4), scales=scl[:], in_=gh[:].rearrange("p w t -> p (w t)"))
+            n = 2 * NB // calls
+            for i in range(calls):
+                nc.vector.quantize_mx(
+                    out=cod[:, n * i : n * (i + 1)].bitcast(FP8X4),
+                    scales=scl[:, n * i : n * (i + 1)],
+                    in_=gh[:, n * i : n * (i + 1), :].rearrange("p w t -> p (w t)"),
+                )
             return cod, scl
 
         def passes(c, h, acc, cod, scl):
@@ -108,39 +129,48 @@ def tile_conditionalfeaturesupsample_w_kernel(tc, local_features, wt, bt, w1_wor
                     for u in range(2):
                         nc.tensor.transpose(xt[:, g2, u, :], x_words[:, 256 * gc + u : 256 * (gc + 1) : 2], ident[:])
                 nc.vector.tensor_copy(out=gx_words[:, 2 * h : 2 * h + 2, :, :], in_=xt[:].rearrange("p g u l -> p g l u"))
-            nc.vector.tensor_copy(out=b1_rows_f[:], in_=b1_rows[:])
-            b1_ps = psum.tile([P, P], F32, tag="bank", name="b1_ps")
-            nc.tensor.transpose(b1_ps[:], b1_rows_f[:], ident[:])
             nc.vector.quantize_mx(
                 out=x_codes[:].rearrange("p g l -> p (g l)").bitcast(FP8X4),
                 scales=x_scales[:].rearrange("p g l -> p (g l)"),
                 in_=gx[:].rearrange("p g l t -> p (g l t)"),
             )
-            nc.vector.tensor_copy(out=b1_f[:], in_=b1_ps[:, 0:NT])
-            nc.vector.tensor_copy(out=bt_f[:], in_=bt_bf[:])
 
-        def turn(acc, last):
+        def turn(go, acc, last):
             up_l = upp.tile([P, 16, P], F32, tag="up_l", name="up_l")
-            for b in range(4):
-                copy = nc.vector.tensor_copy if last and b == 3 else nc.scalar.copy
-                copy(out=up_l[:, :, 32 * b : 32 * (b + 1)], in_=acc[b][:].rearrange("p (q s) -> p s q", s=16))
             banks = []
             for k in range(KS):
                 tb = psum.tile([P, 4, L], F32, tag="bank", name="tb")
-                for j2 in range(4):
-                    nc.tensor.transpose(tb[:, j2, :], up_l[:, 4 * j2 + k, :], ident[:])
+                nc.tensor.matmul(
+                    out=tb[:].rearrange("p j l -> p (j l)"),
+                    lhsT=bt_rows[:],
+                    rhs=pick[:, 4 * go : 4 * go + 4, :].rearrange("p j l -> p (j l)"),
+                    start=True,
+                    stop=False,
+                )
                 banks.append(tb)
+            for b in range(4):
+                copy = nc.vector.tensor_copy if last and b == 3 else nc.scalar.copy
+                copy(out=up_l[:, :, 32 * b : 32 * (b + 1)], in_=acc[b][:].rearrange("p (q s) -> p s q", s=16))
+            for k in range(KS):
+                for j2 in range(4):
+                    nc.tensor.matmul(
+                        out=banks[k][:, j2, :],
+                        lhsT=up_l[:, 4 * j2 + k, :],
+                        rhs=ident[:],
+                        is_transpose=True,
+                        start=False,
+                        stop=(j2 == 3),
+                    )
             return banks
 
-        def finish_up(go, banks):
+        def round_up(go, banks):
             g2t = upp.tile([P, KS, L, 4], BF16, tag="g2t", name="g2t", align_bytes=64)
             for k in range(KS):
-                nc.vector.tensor_tensor(
-                    out=g2t[:, k, :, :],
-                    in0=banks[k][:].rearrange("p j l -> p l j"),
-                    in1=bt_f[:, go, :].unsqueeze(1).to_broadcast([P, L, 4]),
-                    op=ADD,
-                )
+                copy = nc.vector.tensor_copy if go == G - 1 and k % 2 == 1 else nc.scalar.copy
+                copy(out=g2t[:, k, :, :], in_=banks[k][:].rearrange("p j l -> p l j"))
+            return g2t
+
+        def quantise_up(go, g2t):
             nc.vector.quantize_mx(
                 out=up_codes[:, go, :].bitcast(FP8X4),
                 scales=up_scales[:, go, :],
@@ -150,6 +180,7 @@ def tile_conditionalfeaturesupsample_w_kernel(tc, local_features, wt, bt, w1_wor
         acc = [None, None, None, None]
         old_acc = acc
         banks = None
+        g2t = None
         gh_s = None
         waiting = []
         for c in range(CHUNKS + 1):
@@ -157,8 +188,6 @@ def tile_conditionalfeaturesupsample_w_kernel(tc, local_features, wt, bt, w1_wor
                 raw = load_chunk(c)
                 if c == 0:
                     nc.sync.dma_start(out=x_sb[:], in_=local_features[0])
-                    nc.sync.dma_start(out=b1_rows[0:NT, :], in_=b1.rearrange("(n j) -> n j", j=P))
-                    nc.sync.dma_start(out=bt_bf[:], in_=bt.rearrange("(g p j) -> p g j", g=G, p=P, j=4))
                 if c == CHUNKS - 1:
                     for q in range(4):
                         nc.sync.dma_start(
@@ -168,24 +197,22 @@ def tile_conditionalfeaturesupsample_w_kernel(tc, local_features, wt, bt, w1_wor
                     for g in range(G):
                         nc.sync.dma_start(out=w1w[:, g, :].bitcast(I32), in_=w1_src[:, g, :])
                 gh_v = grpp.tile([P, 2 * NB, 4], BF16, tag="gh", name="gh_v", align_bytes=64)
-                if c < 2:
-                    regroup(nc.vector.tensor_copy, raw, gh_v, 0, NB)
-                    regroup(nc.vector.tensor_copy, raw, gh_v, NB, V_COLS)
-                else:
-                    regroup(nc.vector.tensor_copy, raw, gh_v, 0, V_COLS)
+                regroup(nc.vector.tensor_copy, raw, gh_v, 0, 2 * NB)
             if c > 0:
-                waiting.append((c - 1, 1, quantise(gh_s)))
+                waiting.append((c - 1, 1, quantise(gh_s, 2 if c == CHUNKS else 1)))
             if c < CHUNKS:
                 gh_s = grpp.tile([P, 2 * NB, 4], BF16, tag="gh", name="gh_s", align_bytes=64)
-                regroup(nc.scalar.copy, raw, gh_s, 2 * NB, 3 * NB)
-                regroup(nc.scalar.copy, raw, gh_v, V_COLS, 2 * NB)
+                regroup(nc.vector.tensor_copy, raw, gh_s, 2 * NB, V_COLS)
+                regroup(nc.scalar.copy, raw, gh_s, V_COLS, 3 * NB)
                 regroup(nc.scalar.copy, raw, gh_s, 3 * NB, 4 * NB)
             if c == 1:
                 prepare_x()
             if c > 1 and c % G == 1:
-                finish_up(c // G - 1, banks)
+                g2t = round_up(c // G - 1, banks)
+            if c > 2 and c % G == 2:
+                quantise_up(c // G - 1, g2t)
             if c < CHUNKS:
-                waiting.append((c, 0, quantise(gh_v)))
+                waiting.append((c, 0, quantise(gh_v, 1)))
             if c > 0:
                 for cw, h, (cod, scl) in waiting:
                     if cw % G == 0 and h == 0:
@@ -194,8 +221,8 @@ def tile_conditionalfeaturesupsample_w_kernel(tc, local_features, wt, bt, w1_wor
                     passes(cw, h, acc, cod, scl)
                 waiting = []
             if c > 0 and c % G == 0:
-                banks = turn(old_acc if c < CHUNKS else acc, c == CHUNKS)
-        finish_up(G - 1, banks)
+                banks = turn(c // G - 1, old_acc if c < CHUNKS else acc, c == CHUNKS)
+        quantise_up(G - 1, round_up(G - 1, banks))
 
         out_v = out.rearrange("j b n t -> j (b n) t")
         for n in range(NT):

@@ -22,7 +22,8 @@ NT = 16
 W = 2048
 NB = 512
 CHUNKS = G * G
-V_COLS = 1120
+EARLY = 4
+V_COLS = 1088
 
 FLOPS = 2 * L * C * C * KS + 2 * C * C * T
 
@@ -222,12 +223,8 @@ def tile_conditionalfeaturesupsample_w_kernel(tc, local_features, wt, bt, w1_wor
                 waiting = []
             if c > 0 and c % G == 0:
                 banks = turn(c // G - 1, old_acc if c < CHUNKS else acc, c == CHUNKS)
-        quantise_up(G - 1, round_up(G - 1, banks))
-
-        out_v = out.rearrange("j b n t -> j (b n) t")
-        for n in range(NT):
-            ps2 = psum.tile([P, T], F32, tag="bank", name="ps2")
-            for g in range(G):
+        def second_stage(ps2, n, groups):
+            for g in groups:
                 nc.tensor.matmul_mx(
                     out=ps2[:],
                     lhsT=w1w[:, g, P * n : P * (n + 1)].bitcast(FP8X4),
@@ -237,6 +234,22 @@ def tile_conditionalfeaturesupsample_w_kernel(tc, local_features, wt, bt, w1_wor
                     start=(g == 0),
                     stop=(g == G - 1),
                 )
+
+        early = []
+        for n in range(EARLY):
+            ps2 = psum.tile([P, T], F32, tag="bank", name="ps2")
+            second_stage(ps2, n, range(G - 1))
+            early.append(ps2)
+        quantise_up(G - 1, round_up(G - 1, banks))
+
+        out_v = out.rearrange("j b n t -> j (b n) t")
+        for n in range(NT):
+            if n < EARLY:
+                ps2 = early[n]
+                second_stage(ps2, n, [G - 1])
+            else:
+                ps2 = psum.tile([P, T], F32, tag="bank", name="ps2")
+                second_stage(ps2, n, range(G))
             y = outp.tile([P, 2 * T], F32, tag="y", name="y")
             src = ps2[:].rearrange("p (k l) -> p l k", k=KS).unsqueeze(1).to_broadcast([P, 2, L, KS])
             dst = y[:].rearrange("p (r l k) -> p r l k", r=2, k=KS)

@@ -22,8 +22,7 @@ NT = 16
 W = 2048
 NB = 512
 CHUNKS = G * G
-EARLY = 4
-V_COLS = 1088
+V_COLS = 1152
 
 FLOPS = 2 * L * C * C * KS + 2 * C * C * T
 
@@ -223,8 +222,12 @@ def tile_conditionalfeaturesupsample_w_kernel(tc, local_features, wt, bt, w1_wor
                 waiting = []
             if c > 0 and c % G == 0:
                 banks = turn(c // G - 1, old_acc if c < CHUNKS else acc, c == CHUNKS)
-        def second_stage(ps2, n, groups):
-            for g in groups:
+        quantise_up(G - 1, round_up(G - 1, banks))
+
+        out_v = out.rearrange("j b n t -> j (b n) t")
+        for n in range(NT):
+            ps2 = psum.tile([P, T], F32, tag="bank", name="ps2")
+            for g in range(G):
                 nc.tensor.matmul_mx(
                     out=ps2[:],
                     lhsT=w1w[:, g, P * n : P * (n + 1)].bitcast(FP8X4),
@@ -234,22 +237,6 @@ def tile_conditionalfeaturesupsample_w_kernel(tc, local_features, wt, bt, w1_wor
                     start=(g == 0),
                     stop=(g == G - 1),
                 )
-
-        early = []
-        for n in range(EARLY):
-            ps2 = psum.tile([P, T], F32, tag="bank", name="ps2")
-            second_stage(ps2, n, range(G - 1))
-            early.append(ps2)
-        quantise_up(G - 1, round_up(G - 1, banks))
-
-        out_v = out.rearrange("j b n t -> j (b n) t")
-        for n in range(NT):
-            if n < EARLY:
-                ps2 = early[n]
-                second_stage(ps2, n, [G - 1])
-            else:
-                ps2 = psum.tile([P, T], F32, tag="bank", name="ps2")
-                second_stage(ps2, n, range(G))
             y = outp.tile([P, 2 * T], F32, tag="y", name="y")
             src = ps2[:].rearrange("p (k l) -> p l k", k=KS).unsqueeze(1).to_broadcast([P, 2, L, KS])
             dst = y[:].rearrange("p (r l k) -> p r l k", r=2, k=KS)

@@ -22,7 +22,7 @@ NT = 16
 W = 2048
 NB = 512
 CHUNKS = G * G
-V_COLS = 1152
+V_COLS = 1120
 
 FLOPS = 2 * L * C * C * KS + 2 * C * C * T
 
@@ -36,7 +36,7 @@ def tile_conditionalfeaturesupsample_w_kernel(tc, local_features, wt, bt, w1_wor
         grpp = ctx.enter_context(tc.tile_pool(name="grpp", bufs=4))
         codp = ctx.enter_context(tc.tile_pool(name="codp", bufs=4))
         upp = ctx.enter_context(tc.tile_pool(name="upp", bufs=2))
-        outp = ctx.enter_context(tc.tile_pool(name="outp", bufs=5))
+        outp = ctx.enter_context(tc.tile_pool(name="outp", bufs=8))
         psum = ctx.enter_context(tc.psum_pool(name="psum", bufs=8))
 
         planes = keep.tile([P, C], U8, align_bytes=64)

@@ -88,8 +88,8 @@ def tile_conditionalfeaturesupsample_w_kernel(tc, local_features, wt, bt, w1_wor
         def regroup(copy, raw, gh, lo, hi):
             base = lo - lo % (2 * NB)
             copy(
-                out=gh[:, lo - base : hi - base, :].rearrange("p (c i) t -> p c t i", i=4),
-                in_=raw[:, :, lo:hi].rearrange("p t (c i) -> p c t i", i=4),
+                out=gh[:, lo - base : hi - base, :].rearrange("p (c i) t -> p c t i", i=8),
+                in_=raw[:, :, lo:hi].rearrange("p t (c i) -> p c t i", i=8),
             )
 
         def quantise(gh, calls):

@@ -22,7 +22,8 @@ NT = 16
 W = 2048
 NB = 512
 CHUNKS = G * G
-V_COLS = 1120
+HB = 2 * NB
+ID_COLS = 256
 
 FLOPS = 2 * L * C * C * KS + 2 * C * C * T
 
@@ -37,7 +38,9 @@ def tile_conditionalfeaturesupsample_w_kernel(tc, local_features, wt, bt, w1_wor
         codp = ctx.enter_context(tc.tile_pool(name="codp", bufs=4))
         upp = ctx.enter_context(tc.tile_pool(name="upp", bufs=2))
         outp = ctx.enter_context(tc.tile_pool(name="outp", bufs=8))
-        psum = ctx.enter_context(tc.psum_pool(name="psum", bufs=8))
+        accp = ctx.enter_context(tc.psum_pool(name="accp", bufs=1))
+        tbp = ctx.enter_context(tc.psum_pool(name="tbp", bufs=2))
+        idp = ctx.enter_context(tc.psum_pool(name="idp", bufs=2))
 
         planes = keep.tile([P, C], U8, align_bytes=64)
         nc.vector.memset(planes[:].bitcast(I32), 0)
@@ -45,6 +48,8 @@ def tile_conditionalfeaturesupsample_w_kernel(tc, local_features, wt, bt, w1_wor
         nc.vector.memset(b1_rows[:], 0.0)
         ident = keep.tile([P, P], F32)
         make_identity(nc, ident[:])
+        ident_bf = keep.tile([P, P], BF16)
+        nc.vector.tensor_copy(out=ident_bf[:], in_=ident[:])
 
         x_sb = keep.tile([P, C], BF16)
         bt_bf = keep.tile([P, G, 4], BF16)
@@ -67,9 +72,9 @@ def tile_conditionalfeaturesupsample_w_kernel(tc, local_features, wt, bt, w1_wor
         nc.vector.tensor_copy(out=pick[:], in_=ident[:, 0:16].unsqueeze(2).to_broadcast([P, 16, L]))
         nc.vector.tensor_copy(out=bt_pad[:, 0:16], in_=bt_bf[:].rearrange("p g j -> p (g j)"))
         nc.vector.tensor_copy(out=b1_rows_f[:], in_=b1_rows[:])
-        bt_ps = psum.tile([P, P], F32, tag="bank", name="bt_ps")
+        bt_ps = tbp.tile([P, P], F32, tag="tb", name="bt_ps")
         nc.tensor.transpose(bt_ps[:], bt_pad[:], ident[:])
-        b1_ps = psum.tile([P, P], F32, tag="bank", name="b1_ps")
+        b1_ps = tbp.tile([P, P], F32, tag="tb", name="b1_ps")
         nc.tensor.transpose(b1_ps[:], b1_rows_f[:], ident[:])
         nc.vector.tensor_copy(out=bt_rows[:], in_=bt_ps[:])
         nc.vector.tensor_copy(out=b1_f[:], in_=b1_ps[:, 0:NT])
@@ -92,6 +97,19 @@ def tile_conditionalfeaturesupsample_w_kernel(tc, local_features, wt, bt, w1_wor
                 in_=raw[:, :, lo:hi].rearrange("p t (c i) -> p c t i", i=8),
             )
 
+        def spread(raw):
+            bank = idp.tile([P, ID_COLS, 4], BF16, tag="id", name="bank")
+            for i in range(ID_COLS // P):
+                lo = W - ID_COLS + P * i
+                nc.tensor.matmul(
+                    out=bank[:, P * i : P * (i + 1), :],
+                    lhsT=ident_bf[:],
+                    rhs=raw[:, :, lo : lo + P].rearrange("p t c -> p c t"),
+                    start=True,
+                    stop=True,
+                )
+            return bank
+
         def quantise(gh, calls):
             cod = codp.tile([P, 2 * NB], U32, tag="cod", name="cod", align_bytes=64)
             scl = codp.tile([P, 2 * NB], U8, tag="scl", name="scl", align_bytes=64)
@@ -108,7 +126,7 @@ def tile_conditionalfeaturesupsample_w_kernel(tc, local_features, wt, bt, w1_wor
             gc = c % G
             for i in range(2):
                 if gc == 0:
-                    acc[2 * h + i] = psum.tile([P, NB], F32, tag="bank", name="acc")
+                    acc[2 * h + i] = accp.tile([P, NB], F32, tag=f"acc{2 * h + i}", name="acc")
                 nc.tensor.matmul_mx(
                     out=acc[2 * h + i][:],
                     lhsT=x_codes[:, gc, :].bitcast(FP8X4),
@@ -123,7 +141,7 @@ def tile_conditionalfeaturesupsample_w_kernel(tc, local_features, wt, bt, w1_wor
             x_words = x_sb[:].bitcast(F32)
             gx_words = gx[:].bitcast(F32)
             for h in range(2):
-                xt = psum.tile([P, 2, 2, L], F32, tag="bank", name="xt")
+                xt = tbp.tile([P, 2, 2, L], F32, tag="tb", name="xt")
                 for g2 in range(2):
                     gc = 2 * h + g2
                     for u in range(2):
@@ -135,40 +153,31 @@ def tile_conditionalfeaturesupsample_w_kernel(tc, local_features, wt, bt, w1_wor
                 in_=gx[:].rearrange("p g l t -> p (g l t)"),
             )
 
-        def turn(go, acc, last):
-            up_l = upp.tile([P, 16, P], F32, tag="up_l", name="up_l")
-            banks = []
-            for k in range(KS):
-                tb = psum.tile([P, 4, L], F32, tag="bank", name="tb")
-                nc.tensor.matmul(
-                    out=tb[:].rearrange("p j l -> p (j l)"),
-                    lhsT=bt_rows[:],
-                    rhs=pick[:, 4 * go : 4 * go + 4, :].rearrange("p j l -> p (j l)"),
-                    start=True,
-                    stop=False,
-                )
-                banks.append(tb)
-            for b in range(4):
-                copy = nc.vector.tensor_copy if last and b == 3 else nc.scalar.copy
-                copy(out=up_l[:, :, 32 * b : 32 * (b + 1)], in_=acc[b][:].rearrange("p (q s) -> p s q", s=16))
-            for k in range(KS):
-                for j2 in range(4):
-                    nc.tensor.matmul(
-                        out=banks[k][:, j2, :],
-                        lhsT=up_l[:, 4 * j2 + k, :],
-                        rhs=ident[:],
-                        is_transpose=True,
-                        start=False,
-                        stop=(j2 == 3),
-                    )
-            return banks
+        def sort_acc(acc, b, up_l, copy):
+            copy(out=up_l[:, :, 32 * b : 32 * (b + 1)], in_=acc[b][:].rearrange("p (q s) -> p s q", s=16))
 
-        def round_up(go, banks):
-            g2t = upp.tile([P, KS, L, 4], BF16, tag="g2t", name="g2t", align_bytes=64)
-            for k in range(KS):
-                copy = nc.vector.tensor_copy if go == G - 1 and k % 2 == 1 else nc.scalar.copy
-                copy(out=g2t[:, k, :, :], in_=banks[k][:].rearrange("p j l -> p l j"))
-            return g2t
+        def add_bias(go, bank):
+            nc.tensor.matmul(
+                out=bank[:].rearrange("p j l -> p (j l)"),
+                lhsT=bt_rows[:],
+                rhs=pick[:, 4 * go : 4 * go + 4, :].rearrange("p j l -> p (j l)"),
+                start=True,
+                stop=False,
+            )
+
+        def turn(k, up_l, bank):
+            for j2 in range(4):
+                nc.tensor.matmul(
+                    out=bank[:, j2, :],
+                    lhsT=up_l[:, 4 * j2 + k, :],
+                    rhs=ident[:],
+                    is_transpose=True,
+                    start=False,
+                    stop=(j2 == 3),
+                )
+
+        def round_up(k, bank, g2t, copy):
+            copy(out=g2t[:, k, :, :], in_=bank[:].rearrange("p j l -> p l j"))
 
         def quantise_up(go, g2t):
             nc.vector.quantize_mx(
@@ -178,56 +187,77 @@ def tile_conditionalfeaturesupsample_w_kernel(tc, local_features, wt, bt, w1_wor
             )
 
         acc = [None, None, None, None]
-        old_acc = acc
-        banks = None
+        up_l = None
         g2t = None
         gh_s = None
-        waiting = []
-        for c in range(CHUNKS + 1):
-            if c < CHUNKS:
-                raw = load_chunk(c)
-                if c == 0:
-                    nc.sync.dma_start(out=x_sb[:], in_=local_features[0])
-                if c == CHUNKS - 1:
-                    for q in range(4):
-                        nc.sync.dma_start(
-                            out=planes[32 * q : 32 * q + 16, :].bitcast(I32),
-                            in_=w1_scales[:, 4 * q : 4 * q + 4, :].bitcast(I32),
-                        )
-                    for g in range(G):
-                        nc.sync.dma_start(out=w1w[:, g, :].bitcast(I32), in_=w1_src[:, g, :])
-                gh_v = grpp.tile([P, 2 * NB, 4], BF16, tag="gh", name="gh_v", align_bytes=64)
-                regroup(nc.vector.tensor_copy, raw, gh_v, 0, 2 * NB)
-            if c > 0:
-                waiting.append((c - 1, 1, quantise(gh_s, 2 if c == CHUNKS else 1)))
-            if c < CHUNKS:
-                gh_s = grpp.tile([P, 2 * NB, 4], BF16, tag="gh", name="gh_s", align_bytes=64)
-                regroup(nc.vector.tensor_copy, raw, gh_s, 2 * NB, V_COLS)
-                regroup(nc.scalar.copy, raw, gh_s, V_COLS, 3 * NB)
-                regroup(nc.scalar.copy, raw, gh_s, 3 * NB, 4 * NB)
-            if c == 1:
+        bank_next = None
+        raw_next = load_chunk(0)
+        nc.sync.dma_start(out=x_sb[:], in_=local_features[0])
+        for c in range(CHUNKS):
+            go, gc = divmod(c, G)
+            raw = raw_next
+            if c + 1 < CHUNKS:
+                raw_next = load_chunk(c + 1)
+            if c == CHUNKS - 2:
+                for q in range(4):
+                    nc.sync.dma_start(
+                        out=planes[32 * q : 32 * q + 16, :].bitcast(I32),
+                        in_=w1_scales[:, 4 * q : 4 * q + 4, :].bitcast(I32),
+                    )
+                for g in range(G):
+                    nc.sync.dma_start(out=w1w[:, g, :].bitcast(I32), in_=w1_src[:, g, :])
+            bank = spread(raw) if c == 0 else bank_next
+            gh_v = grpp.tile([P, HB, 4], BF16, tag="gh", name="gh_v", align_bytes=64)
+            regroup(nc.vector.tensor_copy, raw, gh_v, 0, HB)
+            gh_old = gh_s
+            gh_s = grpp.tile([P, HB, 4], BF16, tag="gh", name="gh_s", align_bytes=64)
+            regroup(nc.scalar.copy, raw, gh_s, HB, W - ID_COLS)
+            done = quantise(gh_old, 1) if c > 0 else None
+            if c == 0:
                 prepare_x()
-            if c > 1 and c % G == 1:
-                g2t = round_up(c // G - 1, banks)
-            if c > 2 and c % G == 2:
-                quantise_up(c // G - 1, g2t)
-            if c < CHUNKS:
-                waiting.append((c, 0, quantise(gh_v, 1)))
+            if gc == 3 and go > 0:
+                quantise_up(go - 1, g2t)
+            if go > 0 and gc in (1, 2):
+                if gc == 1:
+                    g2t = upp.tile([P, KS, L, 4], BF16, tag="g2t", name="g2t", align_bytes=64)
+                for k in range(2 * gc - 2, 2 * gc):
+                    tb = tbp.tile([P, 4, L], F32, tag="tb", name="tb")
+                    add_bias(go - 1, tb)
+                    turn(k, up_l, tb)
+                    round_up(k, tb, g2t, nc.scalar.copy)
+            codes = quantise(gh_v, 1)
             if c > 0:
-                for cw, h, (cod, scl) in waiting:
-                    if cw % G == 0 and h == 0:
-                        old_acc = acc
-                        acc = [None, None, None, None]
-                    passes(cw, h, acc, cod, scl)
-                waiting = []
-            if c > 0 and c % G == 0:
-                banks = turn(c // G - 1, old_acc if c < CHUNKS else acc, c == CHUNKS)
-        quantise_up(G - 1, round_up(G - 1, banks))
+                passes(c - 1, 1, acc, done[0], done[1])
+            if go > 0 and gc == 0:
+                up_l = upp.tile([P, 16, P], F32, tag="up_l", name="up_l")
+                for b in range(4):
+                    sort_acc(acc, b, up_l, nc.scalar.copy)
+                acc = [None, None, None, None]
+            passes(c, 0, acc, codes[0], codes[1])
+            if c + 1 < CHUNKS:
+                bank_next = spread(raw_next)
+            nc.scalar.copy(out=gh_s[:, HB - ID_COLS : HB, :], in_=bank[:])
 
-        out_v = out.rearrange("j b n t -> j (b n) t")
-        for n in range(NT):
-            ps2 = psum.tile([P, T], F32, tag="bank", name="ps2")
-            for g in range(G):
+        last = G - 1
+        up_l = upp.tile([P, 16, P], F32, tag="up_l", name="up_l")
+        g2t = upp.tile([P, KS, L, 4], BF16, tag="g2t", name="g2t", align_bytes=64)
+        done = quantise(gh_s, 2)
+        for b in range(2):
+            sort_acc(acc, b, up_l, nc.scalar.copy)
+        passes(CHUNKS - 1, 1, acc, done[0], done[1])
+        sort_acc(acc, 2, up_l, nc.scalar.copy)
+        sort_acc(acc, 3, up_l, nc.vector.tensor_copy)
+        banks = [tbp.tile([P, 4, L], F32, tag="tb", name="tb") for k in range(2)]
+        banks += [idp.tile([P, 4, L], F32, tag="id", name="tb") for k in range(2)]
+        for k in range(KS):
+            add_bias(last, banks[k])
+        for k in range(KS):
+            turn(k, up_l, banks[k])
+        for k in range(KS):
+            round_up(k, banks[k], g2t, nc.vector.tensor_copy if k % 2 else nc.scalar.copy)
+
+        def sums(n, ps2, groups):
+            for g in groups:
                 nc.tensor.matmul_mx(
                     out=ps2[:],
                     lhsT=w1w[:, g, P * n : P * (n + 1)].bitcast(FP8X4),
@@ -237,6 +267,27 @@ def tile_conditionalfeaturesupsample_w_kernel(tc, local_features, wt, bt, w1_wor
                     start=(g == 0),
                     stop=(g == G - 1),
                 )
+
+        def sums_bank(n):
+            tag = ("acc0", "acc1", "acc2", "acc3", "tb", "tb", "id", "id")[n % 8]
+            pool = {"acc": accp, "tb": tbp, "id": idp}[tag[:3]]
+            return pool.tile([P, T], F32, tag=tag, name="ps2")
+
+        ahead = []
+        for n in range(4):
+            ps2 = sums_bank(n)
+            sums(n, ps2, range(G - 1))
+            ahead.append(ps2)
+        quantise_up(last, g2t)
+
+        out_v = out.rearrange("j b n t -> j (b n) t")
+        for n in range(NT):
+            if n < 4:
+                ps2 = ahead[n]
+                sums(n, ps2, [G - 1])
+            else:
+                ps2 = sums_bank(n)
+                sums(n, ps2, range(G))
             y = outp.tile([P, 2 * T], F32, tag="y", name="y")
             src = ps2[:].rearrange("p (k l) -> p l k", k=KS).unsqueeze(1).to_broadcast([P, 2, L, KS])
             dst = y[:].rearrange("p (r l k) -> p r l k", r=2, k=KS)

@@ -23,7 +23,8 @@ W = 2048
 NB = 512
 CHUNKS = G * G
 HB = 2 * NB
-ID_COLS = 256
+V_COLS = 1056
+ID_BANK = 184
 
 FLOPS = 2 * L * C * C * KS + 2 * C * C * T
 
@@ -83,11 +84,10 @@ def tile_conditionalfeaturesupsample_w_kernel(tc, local_features, wt, bt, w1_wor
             go, gc = divmod(c, G)
             raw = rawp.tile([P, 4, W], BF16, tag="raw", name="raw")
             src = wt[512 * gc : 512 * (gc + 1), 512 * go : 512 * (go + 1), :].rearrange("(p j) o k -> p j (o k)", j=4)
-            if c < 2:
-                for h in range(2):
-                    nc.sync.dma_start(out=raw[:, :, 2 * NB * h : 2 * NB * (h + 1)], in_=src[:, :, 2 * NB * h : 2 * NB * (h + 1)])
-            else:
-                nc.sync.dma_start(out=raw[:], in_=src)
+            for lo, hi in {0: [(0, NB), (HB, 3 * NB), (NB, HB), (3 * NB, W)], 1: [(0, HB), (HB, W)]}.get(c, [(0, W)]):
+                nc.sync.dma_start(out=raw[:, :, lo:hi], in_=src[:, :, lo:hi])
+                if c == 1 and lo == 0:
+                    nc.sync.dma_start(out=x_sb[:], in_=local_features[0])
             return raw
 
         def regroup(copy, raw, gh, lo, hi):
@@ -98,17 +98,21 @@ def tile_conditionalfeaturesupsample_w_kernel(tc, local_features, wt, bt, w1_wor
             )
 
         def spread(raw):
-            bank = idp.tile([P, ID_COLS, 4], BF16, tag="id", name="bank")
-            for i in range(ID_COLS // P):
-                lo = W - ID_COLS + P * i
-                nc.tensor.matmul(
-                    out=bank[:, P * i : P * (i + 1), :],
-                    lhsT=ident_bf[:],
-                    rhs=raw[:, :, lo : lo + P].rearrange("p t c -> p c t"),
-                    start=True,
-                    stop=True,
-                )
-            return bank
+            banks = []
+            n = ID_BANK // 2
+            for i in range(2):
+                bank = idp.tile([P, ID_BANK, 4], BF16, tag="id", name="bank")
+                for j in range(2):
+                    lo = W + ID_BANK * (i - 2) + n * j
+                    nc.tensor.matmul(
+                        out=bank[:, n * j : n * (j + 1), :],
+                        lhsT=ident_bf[:],
+                        rhs=raw[:, :, lo : lo + n].rearrange("p t c -> p c t"),
+                        start=True,
+                        stop=True,
+                    )
+                banks.append(bank)
+            return banks
 
         def quantise(gh, calls):
             cod = codp.tile([P, 2 * NB], U32, tag="cod", name="cod", align_bytes=64)
@@ -137,7 +141,7 @@ def tile_conditionalfeaturesupsample_w_kernel(tc, local_features, wt, bt, w1_wor
                     stop=(gc == G - 1),
                 )
 
-        def prepare_x():
+        def turn_x():
             x_words = x_sb[:].bitcast(F32)
             gx_words = gx[:].bitcast(F32)
             for h in range(2):
@@ -146,7 +150,9 @@ def tile_conditionalfeaturesupsample_w_kernel(tc, local_features, wt, bt, w1_wor
                     gc = 2 * h + g2
                     for u in range(2):
                         nc.tensor.transpose(xt[:, g2, u, :], x_words[:, 256 * gc + u : 256 * (gc + 1) : 2], ident[:])
-                nc.vector.tensor_copy(out=gx_words[:, 2 * h : 2 * h + 2, :, :], in_=xt[:].rearrange("p g u l -> p g l u"))
+                nc.scalar.copy(out=gx_words[:, 2 * h : 2 * h + 2, :, :], in_=xt[:].rearrange("p g u l -> p g l u"))
+
+        def quantise_x():
             nc.vector.quantize_mx(
                 out=x_codes[:].rearrange("p g l -> p (g l)").bitcast(FP8X4),
                 scales=x_scales[:].rearrange("p g l -> p (g l)"),
@@ -179,20 +185,31 @@ def tile_conditionalfeaturesupsample_w_kernel(tc, local_features, wt, bt, w1_wor
         def round_up(k, bank, g2t, copy):
             copy(out=g2t[:, k, :, :], in_=bank[:].rearrange("p j l -> p l j"))
 
-        def quantise_up(go, g2t):
-            nc.vector.quantize_mx(
-                out=up_codes[:, go, :].bitcast(FP8X4),
-                scales=up_scales[:, go, :],
-                in_=g2t[:].rearrange("p k l j -> p (k l j)"),
-            )
+        def quantise_up(go, g2t, calls=1):
+            n = T // calls
+            for i in range(calls):
+                nc.vector.quantize_mx(
+                    out=up_codes[:, go, n * i : n * (i + 1)].bitcast(FP8X4),
+                    scales=up_scales[:, go, n * i : n * (i + 1)],
+                    in_=g2t[:].rearrange("p k l j -> p (k l j)")[:, 4 * n * i : 4 * n * (i + 1)],
+                )
+
+        def new_up_l():
+            return upp.tile([P, 16, P], F32, tag="up_l", name="up_l")
+
+        def new_g2t():
+            return upp.tile([P, KS, L, 4], BF16, tag="g2t", name="g2t", align_bytes=64)
+
+        def half():
+            return grpp.tile([P, HB, 4], BF16, tag="gh", name="gh", align_bytes=64)
 
         acc = [None, None, None, None]
         up_l = None
         g2t = None
         gh_s = None
-        bank_next = None
+        spread_next = None
+        codes_first = None
         raw_next = load_chunk(0)
-        nc.sync.dma_start(out=x_sb[:], in_=local_features[0])
         for c in range(CHUNKS):
             go, gc = divmod(c, G)
             raw = raw_next
@@ -206,55 +223,68 @@ def tile_conditionalfeaturesupsample_w_kernel(tc, local_features, wt, bt, w1_wor
                     )
                 for g in range(G):
                     nc.sync.dma_start(out=w1w[:, g, :].bitcast(I32), in_=w1_src[:, g, :])
-            bank = spread(raw) if c == 0 else bank_next
-            gh_v = grpp.tile([P, HB, 4], BF16, tag="gh", name="gh_v", align_bytes=64)
-            regroup(nc.vector.tensor_copy, raw, gh_v, 0, HB)
+            spread_now = spread_next
             gh_old = gh_s
-            gh_s = grpp.tile([P, HB, 4], BF16, tag="gh", name="gh_s", align_bytes=64)
-            regroup(nc.scalar.copy, raw, gh_s, HB, W - ID_COLS)
+            if c == 1:
+                turn_x()
+            gh_v = half()
+            gh_s = half()
+            for lo, hi in [(0, NB), (NB, HB)] if c == 0 else [(0, HB)]:
+                regroup(nc.vector.tensor_copy, raw, gh_v, lo, hi)
             done = quantise(gh_old, 1) if c > 0 else None
-            if c == 0:
-                prepare_x()
-            if gc == 3 and go > 0:
-                quantise_up(go - 1, g2t)
-            if go > 0 and gc in (1, 2):
-                if gc == 1:
-                    g2t = upp.tile([P, KS, L, 4], BF16, tag="g2t", name="g2t", align_bytes=64)
-                for k in range(2 * gc - 2, 2 * gc):
+            if go == 0:
+                for lo, hi in [(HB, 3 * NB), (3 * NB, W)] if c == 0 else [(HB, W)]:
+                    regroup(nc.scalar.copy, raw, gh_s, lo, hi)
+            else:
+                regroup(nc.vector.tensor_copy, raw, gh_s, HB, V_COLS)
+                regroup(nc.scalar.copy, raw, gh_s, V_COLS, W - 2 * ID_BANK)
+            if c == 1:
+                quantise_x()
+            if go > 1 and gc == 0:
+                quantise_up(go - 2, g2t)
+            codes = quantise(gh_v, 1)
+            if go > 0 and gc > 1:
+                if gc == 2:
+                    g2t = new_g2t()
+                for k in range(2 * gc - 4, 2 * gc - 2):
                     tb = tbp.tile([P, 4, L], F32, tag="tb", name="tb")
                     add_bias(go - 1, tb)
                     turn(k, up_l, tb)
                     round_up(k, tb, g2t, nc.scalar.copy)
-            codes = quantise(gh_v, 1)
+            if go > 0 and gc == 1:
+                for b in (2, 3):
+                    sort_acc(acc, b, up_l, nc.scalar.copy)
+            if c == 1:
+                passes(0, 0, acc, codes_first[0], codes_first[1])
             if c > 0:
                 passes(c - 1, 1, acc, done[0], done[1])
             if go > 0 and gc == 0:
-                up_l = upp.tile([P, 16, P], F32, tag="up_l", name="up_l")
-                for b in range(4):
+                up_l = new_up_l()
+                for b in (0, 1):
                     sort_acc(acc, b, up_l, nc.scalar.copy)
-                acc = [None, None, None, None]
-            passes(c, 0, acc, codes[0], codes[1])
-            if c + 1 < CHUNKS:
-                bank_next = spread(raw_next)
-            nc.scalar.copy(out=gh_s[:, HB - ID_COLS : HB, :], in_=bank[:])
+            if c == 0:
+                codes_first = codes
+            else:
+                passes(c, 0, acc, codes[0], codes[1])
+            if go > 0:
+                for i in range(2):
+                    lo = HB + ID_BANK * (i - 2)
+                    nc.scalar.copy(out=gh_s[:, lo : lo + ID_BANK, :], in_=spread_now[i][:])
+            if G <= c + 1 < CHUNKS:
+                spread_next = spread(raw_next)
 
         last = G - 1
-        up_l = upp.tile([P, 16, P], F32, tag="up_l", name="up_l")
-        g2t = upp.tile([P, KS, L, 4], BF16, tag="g2t", name="g2t", align_bytes=64)
         done = quantise(gh_s, 2)
-        for b in range(2):
+        up_l = new_up_l()
+        for b in (0, 1):
             sort_acc(acc, b, up_l, nc.scalar.copy)
         passes(CHUNKS - 1, 1, acc, done[0], done[1])
         sort_acc(acc, 2, up_l, nc.scalar.copy)
         sort_acc(acc, 3, up_l, nc.vector.tensor_copy)
+        quantise_up(last - 1, g2t)
+        g2t = new_g2t()
         banks = [tbp.tile([P, 4, L], F32, tag="tb", name="tb") for k in range(2)]
         banks += [idp.tile([P, 4, L], F32, tag="id", name="tb") for k in range(2)]
-        for k in range(KS):
-            add_bias(last, banks[k])
-        for k in range(KS):
-            turn(k, up_l, banks[k])
-        for k in range(KS):
-            round_up(k, banks[k], g2t, nc.vector.tensor_copy if k % 2 else nc.scalar.copy)
 
         def sums(n, ps2, groups):
             for g in groups:
@@ -273,12 +303,21 @@ def tile_conditionalfeaturesupsample_w_kernel(tc, local_features, wt, bt, w1_wor
             pool = {"acc": accp, "tb": tbp, "id": idp}[tag[:3]]
             return pool.tile([P, T], F32, tag=tag, name="ps2")
 
-        ahead = []
-        for n in range(4):
-            ps2 = sums_bank(n)
-            sums(n, ps2, range(G - 1))
-            ahead.append(ps2)
-        quantise_up(last, g2t)
+        for k in range(KS):
+            add_bias(last, banks[k])
+        ahead = [sums_bank(n) for n in range(2)]
+        for n in range(2):
+            sums(n, ahead[n], range(G - 2))
+        for k in range(KS):
+            turn(k, up_l, banks[k])
+        for n in range(2):
+            sums(n, ahead[n], [G - 2])
+        for n in range(2, 4):
+            ahead.append(sums_bank(n))
+            sums(n, ahead[n], range(G - 1))
+        for k in range(KS):
+            round_up(k, banks[k], g2t, nc.vector.tensor_copy if k in (1, 2) else nc.scalar.copy)
+        quantise_up(last, g2t, 2)
 
         out_v = out.rearrange("j b n t -> j (b n) t")
         for n in range(NT):
@@ -291,6 +330,11 @@ def tile_conditionalfeaturesupsample_w_kernel(tc, local_features, wt, bt, w1_wor
             y = outp.tile([P, 2 * T], F32, tag="y", name="y")
             src = ps2[:].rearrange("p (k l) -> p l k", k=KS).unsqueeze(1).to_broadcast([P, 2, L, KS])
             dst = y[:].rearrange("p (r l k) -> p r l k", r=2, k=KS)
+            if n == 0:
+                for r in range(2):
+                    nc.scalar.activation(out=dst[:, r], in_=src[:, r], func=IDENT, bias=b1_f[:, n : n + 1])
+                    nc.sync.dma_start(out=out_v[:, n, T * r : T * (r + 1)], in_=y[:, T * r : T * (r + 1)])
+                continue
             if n % 2 == 0:
                 nc.scalar.activation(out=dst, in_=src, func=IDENT, bias=b1_f[:, n : n + 1])
             else:

@@ -51,6 +51,8 @@ def tile_conditionalfeaturesupsample_w_kernel(tc, local_features, wt, bt, w1_wor
         make_identity(nc, ident[:])
         ident_bf = keep.tile([P, P], BF16)
         nc.vector.tensor_copy(out=ident_bf[:], in_=ident[:])
+        warm = keep.tile([P, 1], F32)
+        nc.scalar.activation(out=warm[:], in_=ident[:, 0:1], func=IDENT)
 
         x_sb = keep.tile([P, C], BF16)
         bt_bf = keep.tile([P, G, 4], BF16)
@@ -71,14 +73,16 @@ def tile_conditionalfeaturesupsample_w_kernel(tc, local_features, wt, bt, w1_wor
         nc.scalar.dma_start(out=bt_bf[:], in_=bt.rearrange("(g p j) -> p g j", g=G, p=P, j=4))
         nc.scalar.dma_start(out=b1_rows[0:NT, :], in_=b1.rearrange("(n j) -> n j", j=P))
         nc.vector.tensor_copy(out=pick[:], in_=ident[:, 0:16].unsqueeze(2).to_broadcast([P, 16, L]))
-        nc.vector.tensor_copy(out=bt_pad[:, 0:16], in_=bt_bf[:].rearrange("p g j -> p (g j)"))
-        nc.vector.tensor_copy(out=b1_rows_f[:], in_=b1_rows[:])
-        bt_ps = tbp.tile([P, P], F32, tag="tb", name="bt_ps")
-        nc.tensor.transpose(bt_ps[:], bt_pad[:], ident[:])
-        b1_ps = tbp.tile([P, P], F32, tag="tb", name="b1_ps")
-        nc.tensor.transpose(b1_ps[:], b1_rows_f[:], ident[:])
-        nc.vector.tensor_copy(out=bt_rows[:], in_=bt_ps[:])
-        nc.vector.tensor_copy(out=b1_f[:], in_=b1_ps[:, 0:NT])
+
+        def turn_biases():
+            nc.scalar.copy(out=bt_pad[:, 0:16], in_=bt_bf[:].rearrange("p g j -> p (g j)"))
+            nc.scalar.copy(out=b1_rows_f[:], in_=b1_rows[:])
+            bt_ps = tbp.tile([P, P], F32, tag="tb", name="bt_ps")
+            nc.tensor.transpose(bt_ps[:], bt_pad[:], ident[:])
+            b1_ps = tbp.tile([P, P], F32, tag="tb", name="b1_ps")
+            nc.tensor.transpose(b1_ps[:], b1_rows_f[:], ident[:])
+            nc.scalar.copy(out=bt_rows[:], in_=bt_ps[:])
+            nc.scalar.copy(out=b1_f[:], in_=b1_ps[:, 0:NT])
 
         def load_chunk(c):
             go, gc = divmod(c, G)
@@ -226,6 +230,7 @@ def tile_conditionalfeaturesupsample_w_kernel(tc, local_features, wt, bt, w1_wor
             spread_now = spread_next
             gh_old = gh_s
             if c == 1:
+                turn_biases()
                 turn_x()
             gh_v = half()
             gh_s = half()

@@ -24,7 +24,7 @@ NB = 512
 CHUNKS = G * G
 HB = 2 * NB
 V_COLS = 1056
-ID_BANK = 184
+ID_BANK = 176
 
 FLOPS = 2 * L * C * C * KS + 2 * C * C * T
 
@@ -109,9 +109,9 @@ def tile_conditionalfeaturesupsample_w_kernel(tc, local_features, wt, bt, w1_wor
                 for j in range(2):
                     lo = W + ID_BANK * (i - 2) + n * j
                     nc.tensor.matmul(
-                        out=bank[:, n * j : n * (j + 1), :],
+                        out=bank[:, n * j : n * (j + 1), :].rearrange("p (c i) t -> p c t i", i=8),
                         lhsT=ident_bf[:],
-                        rhs=raw[:, :, lo : lo + n].rearrange("p t c -> p c t"),
+                        rhs=raw[:, :, lo : lo + n].rearrange("p t (c i) -> p c t i", i=8),
                         start=True,
                         stop=True,
                     )

@@ -38,7 +38,7 @@ def tile_conditionalfeaturesupsample_w_kernel(tc, local_features, wt, bt, w1_wor
         grpp = ctx.enter_context(tc.tile_pool(name="grpp", bufs=4))
         codp = ctx.enter_context(tc.tile_pool(name="codp", bufs=4))
         upp = ctx.enter_context(tc.tile_pool(name="upp", bufs=2))
-        outp = ctx.enter_context(tc.tile_pool(name="outp", bufs=8))
+        outp = ctx.enter_context(tc.tile_pool(name="outp", bufs=4))
         accp = ctx.enter_context(tc.psum_pool(name="accp", bufs=1))
         tbp = ctx.enter_context(tc.psum_pool(name="tbp", bufs=2))
         idp = ctx.enter_context(tc.psum_pool(name="idp", bufs=2))
@@ -70,8 +70,6 @@ def tile_conditionalfeaturesupsample_w_kernel(tc, local_features, wt, bt, w1_wor
         w1w = keep.tile([P, G, C], U32, align_bytes=64)
         w1_src = w1_words.rearrange("g p n t -> p g (n t)").bitcast(I32)
 
-        nc.scalar.dma_start(out=bt_bf[:], in_=bt.rearrange("(g p j) -> p g j", g=G, p=P, j=4))
-        nc.scalar.dma_start(out=b1_rows[0:NT, :], in_=b1.rearrange("(n j) -> n j", j=P))
         nc.vector.tensor_copy(out=pick[:], in_=ident[:, 0:16].unsqueeze(2).to_broadcast([P, 16, L]))
 
         def turn_biases():
@@ -88,7 +86,7 @@ def tile_conditionalfeaturesupsample_w_kernel(tc, local_features, wt, bt, w1_wor
             go, gc = divmod(c, G)
             raw = rawp.tile([P, 4, W], BF16, tag="raw", name="raw")
             src = wt[512 * gc : 512 * (gc + 1), 512 * go : 512 * (go + 1), :].rearrange("(p j) o k -> p j (o k)", j=4)
-            for lo, hi in {0: [(0, NB), (HB, 3 * NB), (NB, HB), (3 * NB, W)], 1: [(0, HB), (HB, W)]}.get(c, [(0, W)]):
+            for lo, hi in {0: [(0, NB), (HB, 3 * NB), (NB, HB), (3 * NB, W)], 1: [(0, HB), (HB, W)], 2: [(0, HB), (HB, W)]}.get(c, [(0, W)]):
                 nc.sync.dma_start(out=raw[:, :, lo:hi], in_=src[:, :, lo:hi])
                 if c == 1 and lo == 0:
                     nc.sync.dma_start(out=x_sb[:], in_=local_features[0])
@@ -225,12 +223,11 @@ def tile_conditionalfeaturesupsample_w_kernel(tc, local_features, wt, bt, w1_wor
                         out=planes[32 * q : 32 * q + 16, :].bitcast(I32),
                         in_=w1_scales[:, 4 * q : 4 * q + 4, :].bitcast(I32),
                     )
-                for g in range(G):
-                    nc.sync.dma_start(out=w1w[:, g, :].bitcast(I32), in_=w1_src[:, g, :])
+                for q in range(4):
+                    nc.sync.dma_start(out=w1w[:, :, NB * q : NB * (q + 1)].bitcast(I32), in_=w1_src[:, :, NB * q : NB * (q + 1)])
             spread_now = spread_next
             gh_old = gh_s
             if c == 1:
-                turn_biases()
                 turn_x()
             gh_v = half()
             gh_s = half()
@@ -241,55 +238,50 @@ def tile_conditionalfeaturesupsample_w_kernel(tc, local_features, wt, bt, w1_wor
                 for lo, hi in [(HB, 3 * NB), (3 * NB, W)] if c == 0 else [(HB, W)]:
                     regroup(nc.scalar.copy, raw, gh_s, lo, hi)
             else:
-                regroup(nc.vector.tensor_copy, raw, gh_s, HB, V_COLS)
-                regroup(nc.scalar.copy, raw, gh_s, V_COLS, W - 2 * ID_BANK)
+                split = V_COLS if c < CHUNKS - 1 else HB
+                if split > HB:
+                    regroup(nc.vector.tensor_copy, raw, gh_s, HB, split)
+                regroup(nc.scalar.copy, raw, gh_s, split, W - 2 * ID_BANK)
+                for i in range(2):
+                    lo = HB + ID_BANK * (i - 2)
+                    nc.scalar.copy(out=gh_s[:, lo : lo + ID_BANK, :], in_=spread_now[i][:])
+            if c == 0:
+                nc.scalar.dma_start(out=bt_bf[:], in_=bt.rearrange("(g p j) -> p g j", g=G, p=P, j=4))
+                nc.scalar.dma_start(out=b1_rows[0:NT, :], in_=b1.rearrange("(n j) -> n j", j=P))
+            if c == 2:
+                turn_biases()
             if c == 1:
                 quantise_x()
-            if go > 1 and gc == 0:
-                quantise_up(go - 2, g2t)
+            if 0 < go < G - 1 and gc == 3:
+                quantise_up(go - 1, g2t)
             codes = quantise(gh_v, 1)
-            if go > 0 and gc > 1:
-                if gc == 2:
+            if go > 0 and gc in (1, 2):
+                if gc == 1:
                     g2t = new_g2t()
-                for k in range(2 * gc - 4, 2 * gc - 2):
+                for k in range(2 * gc - 2, 2 * gc):
                     tb = tbp.tile([P, 4, L], F32, tag="tb", name="tb")
                     add_bias(go - 1, tb)
                     turn(k, up_l, tb)
                     round_up(k, tb, g2t, nc.scalar.copy)
-            if go > 0 and gc == 1:
-                for b in (2, 3):
-                    sort_acc(acc, b, up_l, nc.scalar.copy)
+            if c == CHUNKS - 1:
+                banks = [tbp.tile([P, 4, L], F32, tag="tb", name="tb") for k in range(2)]
+                for k in range(2):
+                    add_bias(go, banks[k])
             if c == 1:
                 passes(0, 0, acc, codes_first[0], codes_first[1])
             if c > 0:
                 passes(c - 1, 1, acc, done[0], done[1])
+            if G <= c + 1 < CHUNKS:
+                spread_next = spread(raw_next)
             if go > 0 and gc == 0:
                 up_l = new_up_l()
-                for b in (0, 1):
+                for b in range(4):
                     sort_acc(acc, b, up_l, nc.scalar.copy)
+                acc = [None, None, None, None]
             if c == 0:
                 codes_first = codes
             else:
                 passes(c, 0, acc, codes[0], codes[1])
-            if go > 0:
-                for i in range(2):
-                    lo = HB + ID_BANK * (i - 2)
-                    nc.scalar.copy(out=gh_s[:, lo : lo + ID_BANK, :], in_=spread_now[i][:])
-            if G <= c + 1 < CHUNKS:
-                spread_next = spread(raw_next)
-
-        last = G - 1
-        done = quantise(gh_s, 2)
-        up_l = new_up_l()
-        for b in (0, 1):
-            sort_acc(acc, b, up_l, nc.scalar.copy)
-        passes(CHUNKS - 1, 1, acc, done[0], done[1])
-        sort_acc(acc, 2, up_l, nc.scalar.copy)
-        sort_acc(acc, 3, up_l, nc.vector.tensor_copy)
-        quantise_up(last - 1, g2t)
-        g2t = new_g2t()
-        banks = [tbp.tile([P, 4, L], F32, tag="tb", name="tb") for k in range(2)]
-        banks += [idp.tile([P, 4, L], F32, tag="id", name="tb") for k in range(2)]
 
         def sums(n, ps2, groups):
             for g in groups:
@@ -308,40 +300,51 @@ def tile_conditionalfeaturesupsample_w_kernel(tc, local_features, wt, bt, w1_wor
             pool = {"acc": accp, "tb": tbp, "id": idp}[tag[:3]]
             return pool.tile([P, T], F32, tag=tag, name="ps2")
 
-        for k in range(KS):
+        last = G - 1
+        done = quantise(gh_s, 2)
+        up_l = new_up_l()
+        for b in (0, 1):
+            sort_acc(acc, b, up_l, nc.scalar.copy)
+        banks += [idp.tile([P, 4, L], F32, tag="id", name="tb") for k in range(2)]
+        for k in range(2, KS):
             add_bias(last, banks[k])
+        passes(CHUNKS - 1, 1, acc, done[0], done[1])
+        sort_acc(acc, 2, up_l, nc.scalar.copy)
+        sort_acc(acc, 3, up_l, nc.vector.tensor_copy)
+        quantise_up(last - 1, g2t)
+        g2t = new_g2t()
         ahead = [sums_bank(n) for n in range(2)]
-        for n in range(2):
-            sums(n, ahead[n], range(G - 2))
+        sums(0, ahead[0], range(2))
         for k in range(KS):
             turn(k, up_l, banks[k])
-        for n in range(2):
-            sums(n, ahead[n], [G - 2])
-        for n in range(2, 4):
-            ahead.append(sums_bank(n))
-            sums(n, ahead[n], range(G - 1))
+        sums(0, ahead[0], range(2, G - 1))
+        sums(1, ahead[1], range(G - 1))
         for k in range(KS):
             round_up(k, banks[k], g2t, nc.vector.tensor_copy if k in (1, 2) else nc.scalar.copy)
         quantise_up(last, g2t, 2)
 
         out_v = out.rearrange("j b n t -> j (b n) t")
         for n in range(NT):
-            if n < 4:
+            if n < 2:
                 ps2 = ahead[n]
                 sums(n, ps2, [G - 1])
             else:
                 ps2 = sums_bank(n)
                 sums(n, ps2, range(G))
-            y = outp.tile([P, 2 * T], F32, tag="y", name="y")
+            if n % 2 == 0:
+                y = outp.tile([P, 2, 2 * T], F32, tag="y", name="y")
             src = ps2[:].rearrange("p (k l) -> p l k", k=KS).unsqueeze(1).to_broadcast([P, 2, L, KS])
-            dst = y[:].rearrange("p (r l k) -> p r l k", r=2, k=KS)
+            dst = y[:, n % 2, :].rearrange("p (r l k) -> p r l k", r=2, k=KS)
             if n == 0:
                 for r in range(2):
                     nc.scalar.activation(out=dst[:, r], in_=src[:, r], func=IDENT, bias=b1_f[:, n : n + 1])
-                    nc.sync.dma_start(out=out_v[:, n, T * r : T * (r + 1)], in_=y[:, T * r : T * (r + 1)])
+                    nc.sync.dma_start(out=out_v[:, n, T * r : T * (r + 1)], in_=y[:, 0, T * r : T * (r + 1)])
                 continue
             if n % 2 == 0:
                 nc.scalar.activation(out=dst, in_=src, func=IDENT, bias=b1_f[:, n : n + 1])
             else:
                 nc.vector.tensor_scalar(out=dst, in0=src, scalar1=b1_f[:, n : n + 1], scalar2=None, op0=ADD)
-            nc.sync.dma_start(out=out_v[:, n, :], in_=y[:])
+            if n == 1 or n >= NT - 2:
+                nc.sync.dma_start(out=out_v[:, n, :], in_=y[:, n % 2, :])
+            elif n % 2 == 1:
+                nc.sync.dma_start(out=out_v[:, n - 1 : n + 1, :], in_=y[:])

@@ -238,7 +238,7 @@ def tile_conditionalfeaturesupsample_w_kernel(tc, local_features, wt, bt, w1_wor
                 for lo, hi in [(HB, 3 * NB), (3 * NB, W)] if c == 0 else [(HB, W)]:
                     regroup(nc.scalar.copy, raw, gh_s, lo, hi)
             else:
-                split = V_COLS if c < CHUNKS - 1 else HB
+                split = V_COLS if gc < 2 else HB
                 if split > HB:
                     regroup(nc.vector.tensor_copy, raw, gh_s, HB, split)
                 regroup(nc.scalar.copy, raw, gh_s, split, W - 2 * ID_BANK)
@@ -313,21 +313,22 @@ def tile_conditionalfeaturesupsample_w_kernel(tc, local_features, wt, bt, w1_wor
         sort_acc(acc, 3, up_l, nc.vector.tensor_copy)
         quantise_up(last - 1, g2t)
         g2t = new_g2t()
-        ahead = [sums_bank(n) for n in range(2)]
+        ahead = [sums_bank(n) for n in range(3)]
         sums(0, ahead[0], range(2))
         for k in range(KS):
             turn(k, up_l, banks[k])
         sums(0, ahead[0], range(2, G - 1))
         sums(1, ahead[1], range(G - 1))
+        sums(2, ahead[2], range(2))
         for k in range(KS):
             round_up(k, banks[k], g2t, nc.vector.tensor_copy if k in (1, 2) else nc.scalar.copy)
         quantise_up(last, g2t, 2)
 
         out_v = out.rearrange("j b n t -> j (b n) t")
         for n in range(NT):
-            if n < 2:
+            if n < 3:
                 ps2 = ahead[n]
-                sums(n, ps2, [G - 1])
+                sums(n, ps2, [G - 1] if n < 2 else range(2, G))
             else:
                 ps2 = sums_bank(n)
                 sums(n, ps2, range(G))

from contextlib import ExitStack

import concourse.mybir as mybir
from concourse.masks import make_identity

BF16 = mybir.dt.bfloat16
F32 = mybir.dt.float32
I32 = mybir.dt.int32
U32 = mybir.dt.uint32
U8 = mybir.dt.uint8
FP8X4 = mybir.dt.float8_e4m3fn_x4
ADD = mybir.AluOpType.add
IDENT = mybir.ActivationFunctionType.Identity

P = 128
L = 128
C = 2048
KS = 4
G = 4
T = L * KS
NT = 16
W = 2048
NB = 512
CHUNKS = G * G
HB = 2 * NB
V_COLS = 1056
ID_BANK = 176

FLOPS = 2 * L * C * C * KS + 2 * C * C * T


def tile_conditionalfeaturesupsample_w_kernel(tc, local_features, wt, bt, w1_words, w1_scales, b1, out):
    nc = tc.nc
    with ExitStack() as ctx:
        ctx.enter_context(tc.manual_schedule())
        keep = ctx.enter_context(tc.tile_pool(name="keep", bufs=1))
        rawp = ctx.enter_context(tc.tile_pool(name="rawp", bufs=4))
        grpp = ctx.enter_context(tc.tile_pool(name="grpp", bufs=4))
        codp = ctx.enter_context(tc.tile_pool(name="codp", bufs=4))
        upp = ctx.enter_context(tc.tile_pool(name="upp", bufs=2))
        outp = ctx.enter_context(tc.tile_pool(name="outp", bufs=4))
        accp = ctx.enter_context(tc.psum_pool(name="accp", bufs=1))
        tbp = ctx.enter_context(tc.psum_pool(name="tbp", bufs=2))
        idp = ctx.enter_context(tc.psum_pool(name="idp", bufs=2))

        planes = keep.tile([P, C], U8, align_bytes=64)
        nc.vector.memset(planes[:].bitcast(I32), 0)
        b1_rows = keep.tile([P, P], BF16)
        nc.vector.memset(b1_rows[:], 0.0)
        ident = keep.tile([P, P], F32)
        make_identity(nc, ident[:])
        ident_bf = keep.tile([P, P], BF16)
        nc.vector.tensor_copy(out=ident_bf[:], in_=ident[:])
        warm = keep.tile([P, 1], F32)
        nc.scalar.activation(out=warm[:], in_=ident[:, 0:1], func=IDENT)

        x_sb = keep.tile([P, C], BF16)
        bt_bf = keep.tile([P, G, 4], BF16)
        bt_pad = keep.tile([P, P], F32)
        nc.vector.memset(bt_pad[:], 0.0)
        bt_rows = keep.tile([P, P], BF16)
        pick = keep.tile([P, 16, L], BF16)
        b1_rows_f = keep.tile([P, P], F32)
        b1_f = keep.tile([P, NT], F32)
        gx = keep.tile([P, G, L, 4], BF16, align_bytes=64)
        x_codes = keep.tile([P, G, L], U32, align_bytes=64)
        x_scales = keep.tile([P, G, L], U8, align_bytes=64)
        up_codes = keep.tile([P, G, T], U32, align_bytes=64)
        up_scales = keep.tile([P, G, T], U8, align_bytes=64)
        w1w = keep.tile([P, G, C], U32, align_bytes=64)
        w1_src = w1_words.rearrange("g p n t -> p g (n t)").bitcast(I32)

        nc.vector.tensor_copy(out=pick[:], in_=ident[:, 0:16].unsqueeze(2).to_broadcast([P, 16, L]))

        def turn_biases():
            nc.scalar.copy(out=bt_pad[:, 0:16], in_=bt_bf[:].rearrange("p g j -> p (g j)"))
            nc.scalar.copy(out=b1_rows_f[:], in_=b1_rows[:])
            bt_ps = tbp.tile([P, P], F32, tag="tb", name="bt_ps")
            nc.tensor.transpose(bt_ps[:], bt_pad[:], ident[:])
            b1_ps = tbp.tile([P, P], F32, tag="tb", name="b1_ps")
            nc.tensor.transpose(b1_ps[:], b1_rows_f[:], ident[:])
            nc.scalar.copy(out=bt_rows[:], in_=bt_ps[:])
            nc.scalar.copy(out=b1_f[:], in_=b1_ps[:, 0:NT])

        def load_chunk(c):
            go, gc = divmod(c, G)
            raw = rawp.tile([P, 4, W], BF16, tag="raw", name="raw")
            src = wt[512 * gc : 512 * (gc + 1), 512 * go : 512 * (go + 1), :].rearrange("(p j) o k -> p j (o k)", j=4)
            for lo, hi in {0: [(0, NB), (HB, 3 * NB), (NB, HB), (3 * NB, W)], 1: [(0, HB), (HB, W)], 2: [(0, HB), (HB, W)]}.get(c, [(0, W)]):
                nc.sync.dma_start(out=raw[:, :, lo:hi], in_=src[:, :, lo:hi])
                if c == 1 and lo == 0:
                    nc.sync.dma_start(out=x_sb[:], in_=local_features[0])
            return raw

        def regroup(copy, raw, gh, lo, hi):
            base = lo - lo % (2 * NB)
            copy(
                out=gh[:, lo - base : hi - base, :].rearrange("p (c i) t -> p c t i", i=8),
                in_=raw[:, :, lo:hi].rearrange("p t (c i) -> p c t i", i=8),
            )

        def spread(raw):
            banks = []
            n = ID_BANK // 2
            for i in range(2):
                bank = idp.tile([P, ID_BANK, 4], BF16, tag="id", name="bank")
                for j in range(2):
                    lo = W + ID_BANK * (i - 2) + n * j
                    nc.tensor.matmul(
                        out=bank[:, n * j : n * (j + 1), :].rearrange("p (c i) t -> p c t i", i=8),
                        lhsT=ident_bf[:],
                        rhs=raw[:, :, lo : lo + n].rearrange("p t (c i) -> p c t i", i=8),
                        start=True,
                        stop=True,
                    )
                banks.append(bank)
            return banks

        def quantise(gh, calls):
            cod = codp.tile([P, 2 * NB], U32, tag="cod", name="cod", align_bytes=64)
            scl = codp.tile([P, 2 * NB], U8, tag="scl", name="scl", align_bytes=64)
            n = 2 * NB // calls
            for i in range(calls):
                nc.vector.quantize_mx(
                    out=cod[:, n * i : n * (i + 1)].bitcast(FP8X4),
                    scales=scl[:, n * i : n * (i + 1)],
                    in_=gh[:, n * i : n * (i + 1), :].rearrange("p w t -> p (w t)"),
                )
            return cod, scl

        def passes(c, h, acc, cod, scl):
            gc = c % G
            for i in range(2):
                if gc == 0:
                    acc[2 * h + i] = accp.tile([P, NB], F32, tag=f"acc{2 * h + i}", name="acc")
                nc.tensor.matmul_mx(
                    out=acc[2 * h + i][:],
                    lhsT=x_codes[:, gc, :].bitcast(FP8X4),
                    lhsT_scale=x_scales[:, gc, :],
                    rhs=cod[:, NB * i : NB * (i + 1)].bitcast(FP8X4),
                    rhs_scale=scl[:, NB * i : NB * (i + 1)],
                    start=(gc == 0),
                    stop=(gc == G - 1),
                )

        def turn_x():
            x_words = x_sb[:].bitcast(F32)
            gx_words = gx[:].bitcast(F32)
            for h in range(2):
                xt = tbp.tile([P, 2, 2, L], F32, tag="tb", name="xt")
                for g2 in range(2):
                    gc = 2 * h + g2
                    for u in range(2):
                        nc.tensor.transpose(xt[:, g2, u, :], x_words[:, 256 * gc + u : 256 * (gc + 1) : 2], ident[:])
                nc.scalar.copy(out=gx_words[:, 2 * h : 2 * h + 2, :, :], in_=xt[:].rearrange("p g u l -> p g l u"))

        def quantise_x():
            nc.vector.quantize_mx(
                out=x_codes[:].rearrange("p g l -> p (g l)").bitcast(FP8X4),
                scales=x_scales[:].rearrange("p g l -> p (g l)"),
                in_=gx[:].rearrange("p g l t -> p (g l t)"),
            )

        def sort_acc(acc, b, up_l, copy):
            copy(out=up_l[:, :, 32 * b : 32 * (b + 1)], in_=acc[b][:].rearrange("p (q s) -> p s q", s=16))

        def add_bias(go, bank):
            nc.tensor.matmul(
                out=bank[:].rearrange("p j l -> p (j l)"),
                lhsT=bt_rows[:],
                rhs=pick[:, 4 * go : 4 * go + 4, :].rearrange("p j l -> p (j l)"),
                start=True,
                stop=False,
            )

        def turn(k, up_l, bank):
            for j2 in range(4):
                nc.tensor.matmul(
                    out=bank[:, j2, :],
                    lhsT=up_l[:, 4 * j2 + k, :],
                    rhs=ident[:],
                    is_transpose=True,
                    start=False,
                    stop=(j2 == 3),
                )

        def round_up(k, bank, g2t, copy):
            copy(out=g2t[:, k, :, :], in_=bank[:].rearrange("p j l -> p l j"))

        def quantise_up(go, g2t, calls=1):
            n = T // calls
            for i in range(calls):
                nc.vector.quantize_mx(
                    out=up_codes[:, go, n * i : n * (i + 1)].bitcast(FP8X4),
                    scales=up_scales[:, go, n * i : n * (i + 1)],
                    in_=g2t[:].rearrange("p k l j -> p (k l j)")[:, 4 * n * i : 4 * n * (i + 1)],
                )

        def new_up_l():
            return upp.tile([P, 16, P], F32, tag="up_l", name="up_l")

        def new_g2t():
            return upp.tile([P, KS, L, 4], BF16, tag="g2t", name="g2t", align_bytes=64)

        def half():
            return grpp.tile([P, HB, 4], BF16, tag="gh", name="gh", align_bytes=64)

        acc = [None, None, None, None]
        up_l = None
        g2t = None
        gh_s = None
        spread_next = None
        codes_first = None
        raw_next = load_chunk(0)
        for c in range(CHUNKS):
            go, gc = divmod(c, G)
            raw = raw_next
            if c + 1 < CHUNKS:
                raw_next = load_chunk(c + 1)
            if c == CHUNKS - 2:
                for q in range(4):
                    nc.sync.dma_start(
                        out=planes[32 * q : 32 * q + 16, :].bitcast(I32),
                        in_=w1_scales[:, 4 * q : 4 * q + 4, :].bitcast(I32),
                    )
                for q in range(4):
                    nc.sync.dma_start(out=w1w[:, :, NB * q : NB * (q + 1)].bitcast(I32), in_=w1_src[:, :, NB * q : NB * (q + 1)])
            spread_now = spread_next
            gh_old = gh_s
            if c == 1:
                turn_x()
            gh_v = half()
            gh_s = half()
            for lo, hi in [(0, NB), (NB, HB)] if c == 0 else [(0, HB)]:
                regroup(nc.vector.tensor_copy, raw, gh_v, lo, hi)
            done = quantise(gh_old, 1) if c > 0 else None
            if go == 0:
                for lo, hi in [(HB, 3 * NB), (3 * NB, W)] if c == 0 else [(HB, W)]:
                    regroup(nc.scalar.copy, raw, gh_s, lo, hi)
            else:
                split = V_COLS if gc < 2 else HB
                if split > HB:
                    regroup(nc.vector.tensor_copy, raw, gh_s, HB, split)
                regroup(nc.scalar.copy, raw, gh_s, split, W - 2 * ID_BANK)
                for i in range(2):
                    lo = HB + ID_BANK * (i - 2)
                    nc.scalar.copy(out=gh_s[:, lo : lo + ID_BANK, :], in_=spread_now[i][:])
            if c == 0:
                nc.scalar.dma_start(out=bt_bf[:], in_=bt.rearrange("(g p j) -> p g j", g=G, p=P, j=4))
                nc.scalar.dma_start(out=b1_rows[0:NT, :], in_=b1.rearrange("(n j) -> n j", j=P))
            if c == 2:
                turn_biases()
            if c == 1:
                quantise_x()
            if 0 < go < G - 1 and gc == 3:
                quantise_up(go - 1, g2t)
            codes = quantise(gh_v, 1)
            if go > 0 and gc in (1, 2):
                if gc == 1:
                    g2t = new_g2t()
                for k in range(2 * gc - 2, 2 * gc):
                    tb = tbp.tile([P, 4, L], F32, tag="tb", name="tb")
                    add_bias(go - 1, tb)
                    turn(k, up_l, tb)
                    round_up(k, tb, g2t, nc.scalar.copy)
            if c == CHUNKS - 1:
                banks = [tbp.tile([P, 4, L], F32, tag="tb", name="tb") for k in range(2)]
                for k in range(2):
                    add_bias(go, banks[k])
            if c == 1:
                passes(0, 0, acc, codes_first[0], codes_first[1])
            if c > 0:
                passes(c - 1, 1, acc, done[0], done[1])
            if G <= c + 1 < CHUNKS:
                spread_next = spread(raw_next)
            if go > 0 and gc == 0:
                up_l = new_up_l()
                for b in range(4):
                    sort_acc(acc, b, up_l, nc.scalar.copy)
                acc = [None, None, None, None]
            if c == 0:
                codes_first = codes
            else:
                passes(c, 0, acc, codes[0], codes[1])

        def sums(n, ps2, groups):
            for g in groups:
                nc.tensor.matmul_mx(
                    out=ps2[:],
                    lhsT=w1w[:, g, P * n : P * (n + 1)].bitcast(FP8X4),
                    lhsT_scale=planes[4 * g : P, P * n : P * (n + 1)],
                    rhs=up_codes[:, g, :].bitcast(FP8X4),
                    rhs_scale=up_scales[:, g, :],
                    start=(g == 0),
                    stop=(g == G - 1),
                )

        def sums_bank(n):
            tag = ("acc0", "acc1", "acc2", "acc3", "tb", "tb", "id", "id")[n % 8]
            pool = {"acc": accp, "tb": tbp, "id": idp}[tag[:3]]
            return pool.tile([P, T], F32, tag=tag, name="ps2")

        last = G - 1
        done = quantise(gh_s, 2)
        up_l = new_up_l()
        for b in (0, 1):
            sort_acc(acc, b, up_l, nc.scalar.copy)
        banks += [idp.tile([P, 4, L], F32, tag="id", name="tb") for k in range(2)]
        for k in range(2, KS):
            add_bias(last, banks[k])
        passes(CHUNKS - 1, 1, acc, done[0], done[1])
        sort_acc(acc, 2, up_l, nc.scalar.copy)
        sort_acc(acc, 3, up_l, nc.vector.tensor_copy)
        quantise_up(last - 1, g2t)
        g2t = new_g2t()
        ahead = [sums_bank(n) for n in range(3)]
        sums(0, ahead[0], range(2))
        for k in range(KS):
            turn(k, up_l, banks[k])
        sums(0, ahead[0], range(2, G - 1))
        sums(1, ahead[1], range(G - 1))
        sums(2, ahead[2], range(2))
        for k in range(KS):
            round_up(k, banks[k], g2t, nc.vector.tensor_copy if k in (1, 2) else nc.scalar.copy)
        quantise_up(last, g2t, 2)

        out_v = out.rearrange("j b n t -> j (b n) t")
        for n in range(NT):
            if n < 3:
                ps2 = ahead[n]
                sums(n, ps2, [G - 1] if n < 2 else range(2, G))
            else:
                ps2 = sums_bank(n)
                sums(n, ps2, range(G))
            if n % 2 == 0:
                y = outp.tile([P, 2, 2 * T], F32, tag="y", name="y")
            src = ps2[:].rearrange("p (k l) -> p l k", k=KS).unsqueeze(1).to_broadcast([P, 2, L, KS])
            dst = y[:, n % 2, :].rearrange("p (r l k) -> p r l k", r=2, k=KS)
            if n == 0:
                for r in range(2):
                    nc.scalar.activation(out=dst[:, r], in_=src[:, r], func=IDENT, bias=b1_f[:, n : n + 1])
                    nc.sync.dma_start(out=out_v[:, n, T * r : T * (r + 1)], in_=y[:, 0, T * r : T * (r + 1)])
                continue
            if n % 2 == 0:
                nc.scalar.activation(out=dst, in_=src, func=IDENT, bias=b1_f[:, n : n + 1])
            else:
                nc.vector.tensor_scalar(out=dst, in0=src, scalar1=b1_f[:, n : n + 1], scalar2=None, op0=ADD)
            if n == 1 or n >= NT - 2:
                nc.sync.dma_start(out=out_v[:, n, :], in_=y[:, n % 2, :])
            elif n % 2 == 1:
                nc.sync.dma_start(out=out_v[:, n - 1 : n + 1, :], in_=y[:])
